import numpy as np
import ml_dtypes


def mxq(x, axis, fmt="e4m3"):
    dtype, down = {"e4m3": (ml_dtypes.float8_e4m3fn, 7), "e5m2": (ml_dtypes.float8_e5m2, 14)}[fmt]
    v = np.moveaxis(np.asarray(x, np.float32).astype(ml_dtypes.bfloat16).astype(np.float64), axis, -1)
    blocks = v.reshape(v.shape[:-1] + (-1, 32))
    amax = np.abs(blocks).max(-1, keepdims=True)
    byte = np.maximum(np.where(amax > 0, np.frexp(amax)[1] - 1 + 127, 0) - down, 1)
    scale = np.exp2(byte - 127.0)
    codes = (blocks / scale).astype(np.float32).astype(dtype).astype(np.float64)
    return np.moveaxis((codes * scale).reshape(v.shape), -1, axis)


WIDE = False


def mx_kscale(k):
    if not WIDE:
        return np.ones(k)
    levels = np.array([10, -10, 5, -5, 0])
    a = np.random.permutation(np.resize(levels, k // 512 * 4)).reshape(k // 512, 4)
    idx = np.arange(k)
    return np.exp2(a[idx // 512, idx % 128 // 32])


BF16 = ml_dtypes.bfloat16


def bf(x):
    return np.asarray(x, np.float32).astype(BF16)


def f64(x):
    return np.asarray(x).astype(np.float64)


B, L, C, H, BLK = 2, 512, 1024, 16, 128
D = C // H
MAX_SCALE_MUL = np.log(100.0)
EPS = 1e-12


def l2norm(t):
    n = np.sqrt(np.sum(t * t, axis=-1, keepdims=True))
    return t / np.maximum(n, EPS)


def setup_inputs():
    s = mx_kscale(C)
    lsm = np.linspace(np.log(4.0), MAX_SCALE_MUL + 1.0, H) + 0.05 * np.random.standard_normal(H)
    return {"x": bf(np.random.standard_normal((B, L, C)) * s),
            "W_qkv": bf(np.random.standard_normal((3 * C, C)) / np.sqrt(C) / s[None, :]),
            "q_bias": bf(np.random.standard_normal(C) * 0.3),
            "v_bias": bf(np.random.standard_normal(C) * 0.3),
            "log_scale_mul": bf(lsm.reshape(1, H, 1, 1))}


def reference(x, W_qkv, q_bias, v_bias, log_scale_mul):
    qb = f64(q_bias)
    bias = np.concatenate([qb, np.zeros_like(qb), f64(v_bias)])
    qkv = (mxq(f64(x), 2, "e4m3") @ mxq(f64(W_qkv), 1, "e4m3").T) + bias
    qkv = qkv.reshape(B, L, 3, H, D)
    q, k, v = np.moveaxis(qkv, 2, 0)
    q = np.swapaxes(q, 1, 2)
    k = np.swapaxes(k, 1, 2)
    v = np.swapaxes(v, 1, 2)
    scale_mul = np.exp(np.minimum(f64(log_scale_mul), MAX_SCALE_MUL))
    q = l2norm(q) * scale_mul
    k = l2norm(k)
    return q, k, v

@@ -1,0 +1,301 @@
+from contextlib import ExitStack
+
+import concourse.mybir as mybir
+from concourse.masks import make_identity
+
+F32 = mybir.dt.float32
+BF16 = mybir.dt.bfloat16
+U32 = mybir.dt.uint32
+U8 = mybir.dt.uint8
+FP8X4 = mybir.dt.float8_e4m3fn_x4
+ALU = mybir.AluOpType
+ACT = mybir.ActivationFunctionType
+
+P = 128
+BATCH = 2
+TOKENS = 512
+FEATURES_IN = 1024
+HEADS = 16
+HEAD_DIM = 64
+SECTION = HEADS * HEAD_DIM
+K_PASS = 512
+PASSES = FEATURES_IN // K_PASS
+ROWS = 512
+BLOCKS = ROWS // P
+WORDS = FEATURES_IN // 2
+CHUNKS = 3 * SECTION // ROWS
+CHUNK_HEADS = ROWS // HEAD_DIM
+Q_SECTION, K_SECTION, V_SECTION = 0, 1, 2
+MAX_SCALE_MUL = 100.0
+EPS = 1e-12
+
+FLOPS = 2 * BATCH * TOKENS * FEATURES_IN * 3 * SECTION
+
+
+def by_head(columns):
+    return columns.rearrange("p (h d) -> p h d", d=HEAD_DIM)
+
+
+def tile_selfattention_pa_kernel(
+    tc, x, W_qkv, q_bias, v_bias, log_scale_mul, out_0, out_1, out_2
+):
+    nc = tc.nc
+    outs = (out_0, out_1, out_2)
+    halves = CHUNKS // 3
+    with ExitStack() as ctx:
+        ctx.enter_context(tc.manual_schedule())
+        keep = ctx.enter_context(tc.tile_pool(name="keep", bufs=1))
+        stage = ctx.enter_context(tc.tile_pool(name="stage", bufs=2))
+        results = ctx.enter_context(tc.tile_pool(name="results", bufs=6))
+        small = ctx.enter_context(tc.tile_pool(name="small", bufs=3))
+        psum = ctx.enter_context(tc.psum_pool(name="psum", bufs=4))
+
+        def x_rows(b):
+            return x[b].rearrange("(p j) k -> p j k", j=BLOCKS)
+
+        def w_rows(section, half):
+            first = section * SECTION + half * ROWS
+            return W_qkv[first : first + ROWS, :].rearrange("(t p) k -> p t k", p=P)
+
+        sources = [
+            x_rows(0),
+            w_rows(V_SECTION, 0),
+            x_rows(1),
+            w_rows(V_SECTION, 1),
+            w_rows(K_SECTION, 0),
+            w_rows(Q_SECTION, 0),
+            w_rows(K_SECTION, 1),
+            w_rows(Q_SECTION, 1),
+        ]
+        x_group = {0: 0, 1: 2}
+        w_group = {
+            (V_SECTION, 0): 1,
+            (V_SECTION, 1): 3,
+            (K_SECTION, 0): 4,
+            (Q_SECTION, 0): 5,
+            (K_SECTION, 1): 6,
+            (Q_SECTION, 1): 7,
+        }
+        raw, codes, scales = [], [], []
+        for i in range(len(sources)):
+            raw.append(keep.tile([P, BLOCKS, FEATURES_IN], BF16, name="raw%d" % i))
+            codes.append(keep.tile([P, PASSES, ROWS], U32, name="codes%d" % i, align_bytes=64))
+            scales.append(keep.tile([P, PASSES, ROWS], U8, name="scales%d" % i, align_bytes=64))
+
+        const_row = keep.tile([P, 2 * SECTION + ROWS], BF16)
+        nc.vector.memset(const_row[:], 0.0)
+        ones = keep.tile([P, P], BF16)
+        nc.vector.memset(ones[:], 1.0)
+        ident = keep.tile([P, P], F32)
+        make_identity(nc, ident[:])
+
+        for i in range(len(sources)):
+            for t in range(BLOCKS):
+                nc.sync.dma_start(out=raw[i][:, t, :], in_=sources[i][:, t, :])
+            if i == 0:
+                nc.sync.dma_start(
+                    out=const_row[0:1, 0:SECTION], in_=q_bias.rearrange("(o n) -> o n", o=1)
+                )
+                nc.sync.dma_start(
+                    out=const_row[0:1, SECTION : 2 * SECTION],
+                    in_=v_bias.rearrange("(o n) -> o n", o=1),
+                )
+                nc.sync.dma_start(
+                    out=const_row[0:1, 2 * SECTION : 2 * SECTION + HEADS],
+                    in_=log_scale_mul.rearrange("o h a b -> o (h a b)"),
+                )
+
+        grouped = {}
+
+        def flip(i):
+            raw_words = raw[i][:].bitcast(F32)
+            values = stage.tile([P, PASSES * ROWS * 4], BF16, align_bytes=64)
+            grouped[i] = values
+            words = values[:].bitcast(F32).rearrange("p (g c u) -> p g c u", g=PASSES, u=2)
+            for t in range(BLOCKS):
+                flipped = psum.tile([P, WORDS // P, P], F32, tag="hold")
+                for gu in range(WORDS // P):
+                    nc.tensor.transpose(
+                        flipped[:, gu, :], raw_words[:, t, gu * P : (gu + 1) * P], ident[:]
+                    )
+                nc.scalar.copy(
+                    out=words[:, :, t * P : (t + 1) * P, :],
+                    in_=flipped[:].rearrange("p (g u) c -> p g c u", u=2),
+                )
+
+        def quantise(i):
+            if i < len(sources):
+                nc.vector.quantize_mx(
+                    out=codes[i][:].rearrange("p g c -> p (g c)").bitcast(FP8X4),
+                    scales=scales[i][:].rearrange("p g c -> p (g c)"),
+                    in_=grouped[i][:],
+                )
+
+        def spread_constants():
+            for i in range(2 * SECTION // ROWS + 1):
+                spread = psum.tile([P, ROWS], F32, tag="pass")
+                nc.tensor.matmul(
+                    out=spread[:],
+                    lhsT=ones[:],
+                    rhs=const_row[:, i * ROWS : (i + 1) * ROWS],
+                    start=True,
+                    stop=True,
+                )
+                if i < 2 * SECTION // ROWS:
+                    nc.vector.tensor_copy(out=bias[:, i * ROWS : (i + 1) * ROWS], in_=spread[:])
+                else:
+                    nc.scalar.activation(out=scale_mul[:], in_=spread[:, 0:HEADS], func=ACT.Exp)
+                    nc.vector.tensor_scalar_min(
+                        out=scale_mul[:], in0=scale_mul[:], scalar1=MAX_SCALE_MUL
+                    )
+
+        bias = keep.tile([P, 2 * SECTION], F32)
+        scale_mul = keep.tile([P, HEADS], F32)
+
+        def product(b, section, half, j, tag):
+            xg = x_group[b]
+            wg = w_group[(section, half)]
+            acc = psum.tile([P, ROWS], F32, tag=tag)
+            for g in range(PASSES):
+                nc.tensor.matmul_mx(
+                    out=acc[:],
+                    lhsT=codes[xg][:, g, j * P : (j + 1) * P].bitcast(FP8X4),
+                    lhsT_scale=scales[xg][:, g, j * P : (j + 1) * P],
+                    rhs=codes[wg][:, g, :].bitcast(FP8X4),
+                    rhs_scale=scales[wg][:, g, :],
+                    start=(g == 0),
+                    stop=(g == PASSES - 1),
+                )
+            return acc
+
+        def add_bias(result, j, acc, first_column):
+            nc.vector.tensor_tensor(
+                out=result[:, :, j, :],
+                in0=by_head(acc[:]),
+                in1=by_head(bias[:, first_column : first_column + ROWS]),
+                op=ALU.add,
+            )
+
+        def store(result, section, b, half):
+            first_head = half * CHUNK_HEADS
+            nc.sync.dma_start(
+                out=outs[section][b, first_head : first_head + CHUNK_HEADS].rearrange(
+                    "h (p j) d -> p h (j d)", j=BLOCKS
+                ),
+                in_=result[:].rearrange("p h j d -> p h (j d)"),
+            )
+
+        def sum_squares(sums, j, values):
+            squares = stage.tile([P, CHUNK_HEADS, HEAD_DIM], F32)
+            for h in range(CHUNK_HEADS):
+                nc.scalar.activation(
+                    out=squares[:, h, :],
+                    in_=values[:, h, :],
+                    func=ACT.Square,
+                    accum_out=sums[:, h, j : j + 1],
+                )
+
+        def clamp(sums):
+            nc.vector.tensor_scalar_max(out=sums[:], in0=sums[:], scalar1=EPS * EPS)
+
+        def root(sums):
+            nc.scalar.sqrt(out=sums[:], in_=sums[:])
+
+        def invert(sums):
+            nc.vector.reciprocal(out=sums[:], in_=sums[:])
+
+        def project_values(b, half, next_group):
+            result = results.tile([P, CHUNK_HEADS, BLOCKS, HEAD_DIM], F32, tag="result")
+            for j in range(BLOCKS):
+                acc = product(b, V_SECTION, half, j, "pass")
+                add_bias(result, j, acc, SECTION + half * ROWS)
+                if j == BLOCKS // 2 - 1:
+                    quantise(next_group)
+            store(result, V_SECTION, b, half)
+
+        def finish_queries(waiting):
+            result, factors, b, half = waiting
+            flat = result[:].rearrange("p h j d -> p (h j) d")
+            nc.vector.tensor_tensor(
+                out=flat,
+                in0=flat,
+                in1=factors[:]
+                .rearrange("p h j -> p (h j)")
+                .unsqueeze(2)
+                .to_broadcast([P, CHUNK_HEADS * BLOCKS, HEAD_DIM]),
+                op=ALU.mult,
+            )
+            store(result, Q_SECTION, b, half)
+
+        def query_factors(waiting):
+            result, factors, b, half = waiting
+            first_head = half * CHUNK_HEADS
+            invert(factors)
+            nc.vector.tensor_tensor(
+                out=factors[:],
+                in0=factors[:],
+                in1=scale_mul[:, first_head : first_head + CHUNK_HEADS]
+                .unsqueeze(2)
+                .to_broadcast([P, CHUNK_HEADS, BLOCKS]),
+                op=ALU.mult,
+            )
+
+        def project_queries_and_keys(b, half, next_group, waiting):
+            q_acc = [product(b, Q_SECTION, half, j, "pass") for j in range(BLOCKS)]
+            k_acc = [product(b, K_SECTION, half, j, "hold") for j in range(BLOCKS)]
+            q_result = results.tile([P, CHUNK_HEADS, BLOCKS, HEAD_DIM], F32, tag="result")
+            k_result = results.tile([P, CHUNK_HEADS, BLOCKS, HEAD_DIM], F32, tag="result")
+            q_sums = small.tile([P, CHUNK_HEADS, BLOCKS], F32)
+            k_sums = small.tile([P, CHUNK_HEADS, BLOCKS], F32)
+
+            sum_squares(k_sums, 0, by_head(k_acc[0][:]))
+            sum_squares(k_sums, 1, by_head(k_acc[1][:]))
+            if waiting is not None:
+                root(waiting[1])
+            sum_squares(k_sums, 2, by_head(k_acc[2][:]))
+            sum_squares(k_sums, 3, by_head(k_acc[3][:]))
+
+            for j in range(BLOCKS):
+                add_bias(q_result, j, q_acc[j], half * ROWS)
+            if waiting is not None:
+                query_factors(waiting)
+            clamp(k_sums)
+
+            sum_squares(q_sums, 0, q_result[:, :, 0, :])
+            sum_squares(q_sums, 1, q_result[:, :, 1, :])
+            root(k_sums)
+            sum_squares(q_sums, 2, q_result[:, :, 2, :])
+            sum_squares(q_sums, 3, q_result[:, :, 3, :])
+
+            quantise(next_group)
+            if waiting is not None:
+                finish_queries(waiting)
+            invert(k_sums)
+            for j in range(BLOCKS):
+                nc.vector.tensor_tensor(
+                    out=k_result[:, :, j, :],
+                    in0=by_head(k_acc[j][:]),
+                    in1=k_sums[:, :, j : j + 1].to_broadcast([P, CHUNK_HEADS, HEAD_DIM]),
+                    op=ALU.mult,
+                )
+            store(k_result, K_SECTION, b, half)
+            clamp(q_sums)
+            return (q_result, q_sums, b, half)
+
+        flip(0)
+        spread_constants()
+        flip(1)
+        quantise(0)
+        quantise(1)
+        waiting = None
+        for n in range(2 * BATCH * halves):
+            if n + 2 < len(sources):
+                flip(n + 2)
+            half, b = divmod(n % (BATCH * halves), BATCH)
+            if n < BATCH * halves:
+                project_values(b, half, n + 2)
+            else:
+                waiting = project_queries_and_keys(b, half, n + 2, waiting)
+        root(waiting[1])
+        query_factors(waiting)
+        finish_queries(waiting)

@@ -13,23 +13,24 @@ ACT = mybir.ActivationFunctionType
 
 P = 128
 BATCH = 2
-TOKENS = 512
 FEATURES_IN = 1024
 HEADS = 16
 HEAD_DIM = 64
 SECTION = HEADS * HEAD_DIM
-K_PASS = 512
+PACK = 4
+K_PASS = P * PACK
 PASSES = FEATURES_IN // K_PASS
 ROWS = 512
 BLOCKS = ROWS // P
-WORDS = FEATURES_IN // 2
-CHUNKS = 3 * SECTION // ROWS
+WORD_BLOCKS = FEATURES_IN // 2 // P
+HALVES = SECTION // ROWS
 CHUNK_HEADS = ROWS // HEAD_DIM
 Q_SECTION, K_SECTION, V_SECTION = 0, 1, 2
+GROUPS_PER_HALF = 4
 MAX_SCALE_MUL = 100.0
 EPS = 1e-12
 
-FLOPS = 2 * BATCH * TOKENS * FEATURES_IN * 3 * SECTION
+FLOPS = 2 * BATCH * ROWS * FEATURES_IN * 3 * SECTION
 
 
 def by_head(columns):
@@ -41,132 +42,148 @@ def tile_selfattention_pa_kernel(
 ):
     nc = tc.nc
     outs = (out_0, out_1, out_2)
-    halves = CHUNKS // 3
     with ExitStack() as ctx:
         ctx.enter_context(tc.manual_schedule())
         keep = ctx.enter_context(tc.tile_pool(name="keep", bufs=1))
-        stage = ctx.enter_context(tc.tile_pool(name="stage", bufs=2))
+        stage = ctx.enter_context(tc.tile_pool(name="stage", bufs=4))
+        scratch = ctx.enter_context(tc.tile_pool(name="scratch", bufs=2))
         results = ctx.enter_context(tc.tile_pool(name="results", bufs=6))
         small = ctx.enter_context(tc.tile_pool(name="small", bufs=3))
         psum = ctx.enter_context(tc.psum_pool(name="psum", bufs=4))
 
-        def x_rows(b):
-            return x[b].rearrange("(p j) k -> p j k", j=BLOCKS)
+        def x_group(b):
+            return b * GROUPS_PER_HALF
 
-        def w_rows(section, half):
-            first = section * SECTION + half * ROWS
+        def w_group(section, half):
+            return half * GROUPS_PER_HALF + 1 + section
+
+        def is_x(i):
+            return i % GROUPS_PER_HALF == 0
+
+        def source(i):
+            half, kind = divmod(i, GROUPS_PER_HALF)
+            if is_x(i):
+                return x[half].rearrange("(p j) k -> p j k", j=BLOCKS)
+            first = (kind - 1) * SECTION + half * ROWS
             return W_qkv[first : first + ROWS, :].rearrange("(t p) k -> p t k", p=P)
 
-        sources = [
-            x_rows(0),
-            w_rows(V_SECTION, 0),
-            x_rows(1),
-            w_rows(V_SECTION, 1),
-            w_rows(K_SECTION, 0),
-            w_rows(Q_SECTION, 0),
-            w_rows(K_SECTION, 1),
-            w_rows(Q_SECTION, 1),
-        ]
-        x_group = {0: 0, 1: 2}
-        w_group = {
-            (V_SECTION, 0): 1,
-            (V_SECTION, 1): 3,
-            (K_SECTION, 0): 4,
-            (Q_SECTION, 0): 5,
-            (K_SECTION, 1): 6,
-            (Q_SECTION, 1): 7,
-        }
+        n_groups = BATCH * GROUPS_PER_HALF
         raw, codes, scales = [], [], []
-        for i in range(len(sources)):
+        for i in range(n_groups):
             raw.append(keep.tile([P, BLOCKS, FEATURES_IN], BF16, name="raw%d" % i))
-            codes.append(keep.tile([P, PASSES, ROWS], U32, name="codes%d" % i, align_bytes=64))
-            scales.append(keep.tile([P, PASSES, ROWS], U8, name="scales%d" % i, align_bytes=64))
+            codes.append(keep.tile([P, PASSES * ROWS], U32, name="codes%d" % i, align_bytes=64))
+            scales.append(keep.tile([P, PASSES * ROWS], U8, name="scales%d" % i, align_bytes=64))
 
-        const_row = keep.tile([P, 2 * SECTION + ROWS], BF16)
-        nc.vector.memset(const_row[:], 0.0)
+        bias_row = keep.tile([P, 2 * SECTION], BF16)
+        nc.vector.memset(bias_row[:], 0.0)
         ones = keep.tile([P, P], BF16)
         nc.vector.memset(ones[:], 1.0)
         ident = keep.tile([P, P], F32)
         make_identity(nc, ident[:])
+        log_mul = keep.tile([P, HEADS], BF16)
+        nc.scalar.dma_start(
+            out=log_mul[:],
+            in_=log_scale_mul.rearrange("o h a b -> (o h a b)").partition_broadcast(P),
+        )
+        nc.scalar.dma_start(
+            out=bias_row[0:1, 0:SECTION], in_=q_bias.rearrange("(o n) -> o n", o=1)
+        )
+        nc.scalar.dma_start(
+            out=bias_row[0:1, SECTION : 2 * SECTION], in_=v_bias.rearrange("(o n) -> o n", o=1)
+        )
+        scale_mul = keep.tile([P, HEADS], F32)
+        nc.scalar.activation(out=scale_mul[:], in_=log_mul[:], func=ACT.Exp)
+        warm = keep.tile([P, HEADS], F32)
+        nc.scalar.sqrt(out=warm[:], in_=scale_mul[:])
+        nc.gpsimd.tensor_scalar_min(out=scale_mul[:], in0=scale_mul[:], scalar1=MAX_SCALE_MUL)
 
-        for i in range(len(sources)):
-            for t in range(BLOCKS):
-                nc.sync.dma_start(out=raw[i][:, t, :], in_=sources[i][:, t, :])
-            if i == 0:
-                nc.sync.dma_start(
-                    out=const_row[0:1, 0:SECTION], in_=q_bias.rearrange("(o n) -> o n", o=1)
-                )
-                nc.sync.dma_start(
-                    out=const_row[0:1, SECTION : 2 * SECTION],
-                    in_=v_bias.rearrange("(o n) -> o n", o=1),
-                )
-                nc.sync.dma_start(
-                    out=const_row[0:1, 2 * SECTION : 2 * SECTION + HEADS],
-                    in_=log_scale_mul.rearrange("o h a b -> o (h a b)"),
-                )
+        def load(i, blocks):
+            for t in blocks:
+                nc.sync.dma_start(out=raw[i][:, t, :], in_=source(i)[:, t, :])
 
-        grouped = {}
+        load(0, range(1))
+        load(1, range(BLOCKS))
+        load(0, range(1, BLOCKS))
+        for i in range(2, n_groups):
+            load(i, range(BLOCKS))
 
-        def flip(i):
+        values = {}
+        flipped = {}
+
+        def turn(i, t, tag):
+            if i not in values:
+                values[i] = stage.tile(
+                    [P, PASSES * ROWS * PACK], BF16, name="values%d" % i, tag="values", align_bytes=64
+                )
             raw_words = raw[i][:].bitcast(F32)
-            values = stage.tile([P, PASSES * ROWS * 4], BF16, align_bytes=64)
-            grouped[i] = values
-            words = values[:].bitcast(F32).rearrange("p (g c u) -> p g c u", g=PASSES, u=2)
-            for t in range(BLOCKS):
-                flipped = psum.tile([P, WORDS // P, P], F32, tag="hold")
-                for gu in range(WORDS // P):
-                    nc.tensor.transpose(
-                        flipped[:, gu, :], raw_words[:, t, gu * P : (gu + 1) * P], ident[:]
-                    )
-                nc.scalar.copy(
-                    out=words[:, :, t * P : (t + 1) * P, :],
-                    in_=flipped[:].rearrange("p (g u) c -> p g c u", u=2),
-                )
+            bank = psum.tile([P, WORD_BLOCKS, P], F32, tag=tag)
+            for gu in range(WORD_BLOCKS):
+                columns = slice(gu * P, (gu + 1) * P)
+                nc.tensor.transpose(bank[:, gu, :], raw_words[:, t, columns], ident[:])
+            flipped[(i, t)] = bank
 
-        def quantise(i):
-            if i < len(sources):
+        def collect(copy, i, t):
+            words = values[i][:].bitcast(F32)
+            if is_x(i):
+                target = words.rearrange("p (t g c u) -> p t g c u", t=BLOCKS, g=PASSES, u=2)[:, t]
+            else:
+                target = words.rearrange("p (g c u) -> p g c u", g=PASSES, u=2)[
+                    :, :, t * P : (t + 1) * P, :
+                ]
+            copy(out=target, in_=flipped[(i, t)][:].rearrange("p (g u) c -> p g c u", u=2))
+
+        def flip(i, blocks, tag):
+            for t in blocks:
+                turn(i, t, tag)
+                collect(nc.scalar.copy, i, t)
+
+        def quantise(i, parts):
+            width = PASSES * P if is_x(i) else ROWS
+            for part in parts:
+                words = slice(part * width, (part + 1) * width)
                 nc.vector.quantize_mx(
-                    out=codes[i][:].rearrange("p g c -> p (g c)").bitcast(FP8X4),
-                    scales=scales[i][:].rearrange("p g c -> p (g c)"),
-                    in_=grouped[i][:],
+                    out=codes[i][:, words].bitcast(FP8X4),
+                    scales=scales[i][:, words],
+                    in_=values[i][:, part * width * PACK : (part + 1) * width * PACK],
                 )
 
-        def spread_constants():
-            for i in range(2 * SECTION // ROWS + 1):
-                spread = psum.tile([P, ROWS], F32, tag="pass")
-                nc.tensor.matmul(
-                    out=spread[:],
-                    lhsT=ones[:],
-                    rhs=const_row[:, i * ROWS : (i + 1) * ROWS],
-                    start=True,
-                    stop=True,
-                )
-                if i < 2 * SECTION // ROWS:
-                    nc.vector.tensor_copy(out=bias[:, i * ROWS : (i + 1) * ROWS], in_=spread[:])
-                else:
-                    nc.scalar.activation(out=scale_mul[:], in_=spread[:, 0:HEADS], func=ACT.Exp)
-                    nc.vector.tensor_scalar_min(
-                        out=scale_mul[:], in0=scale_mul[:], scalar1=MAX_SCALE_MUL
-                    )
+        def quantise_all(i):
+            quantise(i, range(BLOCKS if is_x(i) else PASSES))
 
         bias = keep.tile([P, 2 * SECTION], F32)
-        scale_mul = keep.tile([P, HEADS], F32)
 
-        def product(b, section, half, j, tag):
-            xg = x_group[b]
-            wg = w_group[(section, half)]
-            acc = psum.tile([P, ROWS], F32, tag=tag)
-            for g in range(PASSES):
-                nc.tensor.matmul_mx(
-                    out=acc[:],
-                    lhsT=codes[xg][:, g, j * P : (j + 1) * P].bitcast(FP8X4),
-                    lhsT_scale=scales[xg][:, g, j * P : (j + 1) * P],
-                    rhs=codes[wg][:, g, :].bitcast(FP8X4),
-                    rhs_scale=scales[wg][:, g, :],
-                    start=(g == 0),
-                    stop=(g == PASSES - 1),
-                )
-            return acc
+        def spread_bias(i):
+            columns = slice(i * ROWS, (i + 1) * ROWS)
+            spread = psum.tile([P, ROWS], F32, tag="pass")
+            nc.tensor.matmul(
+                out=spread[:], lhsT=ones[:], rhs=bias_row[:, columns], start=True, stop=True
+            )
+            nc.vector.tensor_copy(out=bias[:, columns], in_=spread[:])
+
+        def products(b, section, half, tag):
+            xg = x_group(b)
+            wg = w_group(section, half)
+            banks = []
+            for j in range(BLOCKS):
+                acc = psum.tile([P, ROWS], F32, tag=tag)
+                for g in range(PASSES):
+                    tokens = slice((j * PASSES + g) * P, (j * PASSES + g + 1) * P)
+                    features = slice(g * ROWS, (g + 1) * ROWS)
+                    nc.tensor.matmul_mx(
+                        out=acc[:],
+                        lhsT=codes[xg][:, tokens].bitcast(FP8X4),
+                        lhsT_scale=scales[xg][:, tokens],
+                        rhs=codes[wg][:, features].bitcast(FP8X4),
+                        rhs_scale=scales[wg][:, features],
+                        start=(g == 0),
+                        stop=(g == PASSES - 1),
+                    )
+                banks.append(acc)
+            return banks
+
+        def new_result():
+            result = results.tile([P, CHUNK_HEADS, BLOCKS, HEAD_DIM], F32, tag="result")
+            return result
 
         def add_bias(result, j, acc, first_column):
             nc.vector.tensor_tensor(
@@ -185,12 +202,12 @@ def tile_selfattention_pa_kernel(
                 in_=result[:].rearrange("p h j d -> p h (j d)"),
             )
 
-        def sum_squares(sums, j, values):
-            squares = stage.tile([P, CHUNK_HEADS, HEAD_DIM], F32)
+        def sum_squares(sums, j, features):
+            squares = scratch.tile([P, CHUNK_HEADS, HEAD_DIM], F32)
             for h in range(CHUNK_HEADS):
                 nc.scalar.activation(
                     out=squares[:, h, :],
-                    in_=values[:, h, :],
+                    in_=features[:, h, :],
                     func=ACT.Square,
                     accum_out=sums[:, h, j : j + 1],
                 )
@@ -204,72 +221,9 @@ def tile_selfattention_pa_kernel(
         def invert(sums):
             nc.vector.reciprocal(out=sums[:], in_=sums[:])
 
-        def project_values(b, half, next_group):
-            result = results.tile([P, CHUNK_HEADS, BLOCKS, HEAD_DIM], F32, tag="result")
-            for j in range(BLOCKS):
-                acc = product(b, V_SECTION, half, j, "pass")
-                add_bias(result, j, acc, SECTION + half * ROWS)
-                if j == BLOCKS // 2 - 1:
-                    quantise(next_group)
-            store(result, V_SECTION, b, half)
-
-        def finish_queries(waiting):
-            result, factors, b, half = waiting
-            flat = result[:].rearrange("p h j d -> p (h j) d")
-            nc.vector.tensor_tensor(
-                out=flat,
-                in0=flat,
-                in1=factors[:]
-                .rearrange("p h j -> p (h j)")
-                .unsqueeze(2)
-                .to_broadcast([P, CHUNK_HEADS * BLOCKS, HEAD_DIM]),
-                op=ALU.mult,
-            )
-            store(result, Q_SECTION, b, half)
-
-        def query_factors(waiting):
-            result, factors, b, half = waiting
-            first_head = half * CHUNK_HEADS
-            invert(factors)
-            nc.vector.tensor_tensor(
-                out=factors[:],
-                in0=factors[:],
-                in1=scale_mul[:, first_head : first_head + CHUNK_HEADS]
-                .unsqueeze(2)
-                .to_broadcast([P, CHUNK_HEADS, BLOCKS]),
-                op=ALU.mult,
-            )
-
-        def project_queries_and_keys(b, half, next_group, waiting):
-            q_acc = [product(b, Q_SECTION, half, j, "pass") for j in range(BLOCKS)]
-            k_acc = [product(b, K_SECTION, half, j, "hold") for j in range(BLOCKS)]
-            q_result = results.tile([P, CHUNK_HEADS, BLOCKS, HEAD_DIM], F32, tag="result")
-            k_result = results.tile([P, CHUNK_HEADS, BLOCKS, HEAD_DIM], F32, tag="result")
-            q_sums = small.tile([P, CHUNK_HEADS, BLOCKS], F32)
-            k_sums = small.tile([P, CHUNK_HEADS, BLOCKS], F32)
-
-            sum_squares(k_sums, 0, by_head(k_acc[0][:]))
-            sum_squares(k_sums, 1, by_head(k_acc[1][:]))
-            if waiting is not None:
-                root(waiting[1])
-            sum_squares(k_sums, 2, by_head(k_acc[2][:]))
-            sum_squares(k_sums, 3, by_head(k_acc[3][:]))
-
-            for j in range(BLOCKS):
-                add_bias(q_result, j, q_acc[j], half * ROWS)
-            if waiting is not None:
-                query_factors(waiting)
-            clamp(k_sums)
-
-            sum_squares(q_sums, 0, q_result[:, :, 0, :])
-            sum_squares(q_sums, 1, q_result[:, :, 1, :])
-            root(k_sums)
-            sum_squares(q_sums, 2, q_result[:, :, 2, :])
-            sum_squares(q_sums, 3, q_result[:, :, 3, :])
-
-            quantise(next_group)
-            if waiting is not None:
-                finish_queries(waiting)
+        def finish_keys(waiting):
+            k_acc, k_sums, b, half = waiting
+            k_result = new_result()
             invert(k_sums)
             for j in range(BLOCKS):
                 nc.vector.tensor_tensor(
@@ -279,23 +233,90 @@ def tile_selfattention_pa_kernel(
                     op=ALU.mult,
                 )
             store(k_result, K_SECTION, b, half)
-            clamp(q_sums)
-            return (q_result, q_sums, b, half)
 
-        flip(0)
-        spread_constants()
-        flip(1)
-        quantise(0)
-        quantise(1)
+        def finish_queries(q_result, q_sums, b, half):
+            first_head = half * CHUNK_HEADS
+            invert(q_sums)
+            nc.vector.tensor_tensor(
+                out=q_sums[:],
+                in0=q_sums[:],
+                in1=scale_mul[:, first_head : first_head + CHUNK_HEADS]
+                .unsqueeze(2)
+                .to_broadcast([P, CHUNK_HEADS, BLOCKS]),
+                op=ALU.mult,
+            )
+            flat = q_result[:].rearrange("p h j d -> p (h j) d")
+            nc.vector.tensor_tensor(
+                out=flat,
+                in0=flat,
+                in1=q_sums[:]
+                .rearrange("p h j -> p (h j)")
+                .unsqueeze(2)
+                .to_broadcast([P, CHUNK_HEADS * BLOCKS, HEAD_DIM]),
+                op=ALU.mult,
+            )
+            store(q_result, Q_SECTION, b, half)
+
+        flip(0, range(1), "pass")
+        quantise(0, range(1))
+        for t in range(BLOCKS):
+            flip(1, [t], "hold")
+            spread_bias(t)
+        flip(0, range(1, BLOCKS), "pass")
+        quantise_all(1)
+        quantise(0, range(1, BLOCKS))
+
         waiting = None
-        for n in range(2 * BATCH * halves):
-            if n + 2 < len(sources):
-                flip(n + 2)
-            half, b = divmod(n % (BATCH * halves), BATCH)
-            if n < BATCH * halves:
-                project_values(b, half, n + 2)
-            else:
-                waiting = project_queries_and_keys(b, half, n + 2, waiting)
+        for n in range(BATCH * HALVES):
+            half, b = divmod(n, BATCH)
+            first_round = n == 0
+            ahead = [GROUPS_PER_HALF + 2 * n, GROUPS_PER_HALF + 2 * n + 1] if n < 2 else []
+
+            q_acc = products(b, Q_SECTION, half, "pass")
+            if first_round:
+                for t in range(BLOCKS):
+                    turn(2, t, "hold")
+            if waiting is not None:
+                clamp(waiting[1])
+            q_result = new_result()
+            for j in range(BLOCKS):
+                add_bias(q_result, j, q_acc[j], half * ROWS)
+            q_sums = small.tile([P, CHUNK_HEADS, BLOCKS], F32)
+            for j in range(BLOCKS):
+                sum_squares(q_sums, j, q_result[:, :, j, :])
+                if waiting is not None and j == 0:
+                    root(waiting[1])
+            if first_round:
+                for t in range(BLOCKS):
+                    collect(nc.vector.tensor_copy, 2, t)
+                quantise_all(2)
+                flip(3, range(BLOCKS), "pass")
+            if waiting is not None:
+                finish_keys(waiting)
+
+            k_acc = products(b, K_SECTION, half, "hold")
+            clamp(q_sums)
+            if first_round:
+                quantise_all(3)
+            if n in (1, 2):
+                quantise_all(GROUPS_PER_HALF + 2 * n - 1)
+            v_acc = products(b, V_SECTION, half, "pass")
+            k_sums = small.tile([P, CHUNK_HEADS, BLOCKS], F32)
+            for j in range(BLOCKS):
+                sum_squares(k_sums, j, by_head(k_acc[j][:]))
+                if j == 0:
+                    root(q_sums)
+            v_result = new_result()
+            for j in range(BLOCKS):
+                add_bias(v_result, j, v_acc[j], SECTION + half * ROWS)
+            store(v_result, V_SECTION, b, half)
+            for i in ahead:
+                flip(i, range(BLOCKS), "pass")
+            finish_queries(q_result, q_sums, b, half)
+            if ahead:
+                quantise_all(ahead[0])
+            waiting = (k_acc, k_sums, b, half)
+
+        clamp(waiting[1])
         root(waiting[1])
-        query_factors(waiting)
-        finish_queries(waiting)
+        finish_keys(waiting)

@@ -74,28 +74,24 @@ def tile_selfattention_pa_kernel(
             codes.append(keep.tile([P, PASSES * ROWS], U32, name="codes%d" % i, align_bytes=64))
             scales.append(keep.tile([P, PASSES * ROWS], U8, name="scales%d" % i, align_bytes=64))
 
-        bias_row = keep.tile([P, 2 * SECTION], BF16)
-        nc.vector.memset(bias_row[:], 0.0)
+        const_row = keep.tile([P, 2 * SECTION + ROWS], BF16)
+        nc.vector.memset(const_row[:], 0.0)
         ones = keep.tile([P, P], BF16)
         nc.vector.memset(ones[:], 1.0)
         ident = keep.tile([P, P], F32)
         make_identity(nc, ident[:])
-        log_mul = keep.tile([P, HEADS], BF16)
         nc.scalar.dma_start(
-            out=log_mul[:],
-            in_=log_scale_mul.rearrange("o h a b -> (o h a b)").partition_broadcast(P),
+            out=const_row[0:1, 0:SECTION], in_=q_bias.rearrange("(o n) -> o n", o=1)
         )
         nc.scalar.dma_start(
-            out=bias_row[0:1, 0:SECTION], in_=q_bias.rearrange("(o n) -> o n", o=1)
+            out=const_row[0:1, SECTION : 2 * SECTION], in_=v_bias.rearrange("(o n) -> o n", o=1)
         )
         nc.scalar.dma_start(
-            out=bias_row[0:1, SECTION : 2 * SECTION], in_=v_bias.rearrange("(o n) -> o n", o=1)
+            out=const_row[0:1, 2 * SECTION : 2 * SECTION + HEADS],
+            in_=log_scale_mul.rearrange("o h a b -> o (h a b)"),
         )
-        scale_mul = keep.tile([P, HEADS], F32)
-        nc.scalar.activation(out=scale_mul[:], in_=log_mul[:], func=ACT.Exp)
         warm = keep.tile([P, HEADS], F32)
-        nc.scalar.sqrt(out=warm[:], in_=scale_mul[:])
-        nc.gpsimd.tensor_scalar_min(out=scale_mul[:], in0=scale_mul[:], scalar1=MAX_SCALE_MUL)
+        nc.scalar.activation(out=warm[:], in_=ones[:, 0:HEADS], func=ACT.Exp)
 
         def load(i, blocks):
             for t in blocks:
@@ -151,14 +147,22 @@ def tile_selfattention_pa_kernel(
             quantise(i, range(BLOCKS if is_x(i) else PASSES))
 
         bias = keep.tile([P, 2 * SECTION], F32)
+        scale_mul = keep.tile([P, HEADS], F32)
+
+        def spread(i):
+            bank = psum.tile([P, ROWS], F32, tag="pass")
+            nc.tensor.matmul(
+                out=bank[:],
+                lhsT=ones[:],
+                rhs=const_row[:, i * ROWS : (i + 1) * ROWS],
+                start=True,
+                stop=True,
+            )
+            return bank
 
         def spread_bias(i):
-            columns = slice(i * ROWS, (i + 1) * ROWS)
-            spread = psum.tile([P, ROWS], F32, tag="pass")
-            nc.tensor.matmul(
-                out=spread[:], lhsT=ones[:], rhs=bias_row[:, columns], start=True, stop=True
-            )
-            nc.vector.tensor_copy(out=bias[:, columns], in_=spread[:])
+            bank = spread(i)
+            nc.vector.tensor_copy(out=bias[:, i * ROWS : (i + 1) * ROWS], in_=bank[:])
 
         def products(b, section, half, tag):
             xg = x_group(b)
@@ -259,12 +263,15 @@ def tile_selfattention_pa_kernel(
 
         flip(0, range(1), "pass")
         quantise(0, range(1))
-        for t in range(BLOCKS):
-            flip(1, [t], "hold")
-            spread_bias(t)
+        flip(1, range(BLOCKS), "hold")
+        spread_bias(0)
+        log_mul = spread(2 * SECTION // ROWS)
         flip(0, range(1, BLOCKS), "pass")
         quantise_all(1)
         quantise(0, range(1, BLOCKS))
+        nc.scalar.activation(out=scale_mul[:], in_=log_mul[:, 0:HEADS], func=ACT.Exp)
+        nc.scalar.sqrt(out=warm[:], in_=scale_mul[:])
+        nc.gpsimd.tensor_scalar_min(out=scale_mul[:], in0=scale_mul[:], scalar1=MAX_SCALE_MUL)
 
         waiting = None
         for n in range(BATCH * HALVES):
@@ -291,6 +298,8 @@ def tile_selfattention_pa_kernel(
                     collect(nc.vector.tensor_copy, 2, t)
                 quantise_all(2)
                 flip(3, range(BLOCKS), "pass")
+                for i in range(1, 2 * SECTION // ROWS):
+                    spread_bias(i)
             if waiting is not None:
                 finish_keys(waiting)
 

@@ -238,7 +238,7 @@ def tile_selfattention_pa_kernel(
                 )
             store(k_result, K_SECTION, b, half)
 
-        def finish_queries(q_result, q_sums, b, half):
+        def scale_queries(q_result, q_sums, half):
             first_head = half * CHUNK_HEADS
             invert(q_sums)
             nc.vector.tensor_tensor(
@@ -249,17 +249,17 @@ def tile_selfattention_pa_kernel(
                 .to_broadcast([P, CHUNK_HEADS, BLOCKS]),
                 op=ALU.mult,
             )
-            flat = q_result[:].rearrange("p h j d -> p (h j) d")
-            nc.vector.tensor_tensor(
-                out=flat,
-                in0=flat,
-                in1=q_sums[:]
-                .rearrange("p h j -> p (h j)")
-                .unsqueeze(2)
-                .to_broadcast([P, CHUNK_HEADS * BLOCKS, HEAD_DIM]),
-                op=ALU.mult,
-            )
-            store(q_result, Q_SECTION, b, half)
+            for h in range(0, CHUNK_HEADS, 2):
+                two_heads = q_result[:, h : h + 2].rearrange("p h j d -> p (h j) d")
+                nc.gpsimd.tensor_tensor(
+                    out=two_heads,
+                    in0=two_heads,
+                    in1=q_sums[:, h : h + 2]
+                    .rearrange("p h j -> p (h j)")
+                    .unsqueeze(2)
+                    .to_broadcast([P, 2 * BLOCKS, HEAD_DIM]),
+                    op=ALU.mult,
+                )
 
         flip(0, range(1), "pass")
         quantise(0, range(1))
@@ -274,12 +274,15 @@ def tile_selfattention_pa_kernel(
         nc.gpsimd.tensor_scalar_min(out=scale_mul[:], in0=scale_mul[:], scalar1=MAX_SCALE_MUL)
 
         waiting = None
+        scaling = None
         for n in range(BATCH * HALVES):
             half, b = divmod(n, BATCH)
             first_round = n == 0
             ahead = [GROUPS_PER_HALF + 2 * n, GROUPS_PER_HALF + 2 * n + 1] if n < 2 else []
 
             q_acc = products(b, Q_SECTION, half, "pass")
+            if scaling is not None:
+                store(scaling[0], Q_SECTION, scaling[1], scaling[2])
             if first_round:
                 for t in range(BLOCKS):
                     turn(2, t, "hold")
@@ -315,17 +318,19 @@ def tile_selfattention_pa_kernel(
                 sum_squares(k_sums, j, by_head(k_acc[j][:]))
                 if j == 0:
                     root(q_sums)
+            scale_queries(q_result, q_sums, half)
+            scaling = (q_result, b, half)
             v_result = new_result()
             for j in range(BLOCKS):
                 add_bias(v_result, j, v_acc[j], SECTION + half * ROWS)
             store(v_result, V_SECTION, b, half)
             for i in ahead:
                 flip(i, range(BLOCKS), "pass")
-            finish_queries(q_result, q_sums, b, half)
             if ahead:
                 quantise_all(ahead[0])
             waiting = (k_acc, k_sums, b, half)
 
         clamp(waiting[1])
         root(waiting[1])
+        store(scaling[0], Q_SECTION, scaling[1], scaling[2])
         finish_keys(waiting)

@@ -25,6 +25,7 @@ BLOCKS = ROWS // P
 WORD_BLOCKS = FEATURES_IN // 2 // P
 HALVES = SECTION // ROWS
 CHUNK_HEADS = ROWS // HEAD_DIM
+STORE_HEADS = 4
 Q_SECTION, K_SECTION, V_SECTION = 0, 1, 2
 GROUPS_PER_HALF = 4
 MAX_SCALE_MUL = 100.0
@@ -198,13 +199,14 @@ def tile_selfattention_pa_kernel(
             )
 
         def store(result, section, b, half):
-            first_head = half * CHUNK_HEADS
-            nc.sync.dma_start(
-                out=outs[section][b, first_head : first_head + CHUNK_HEADS].rearrange(
-                    "h (p j) d -> p h (j d)", j=BLOCKS
-                ),
-                in_=result[:].rearrange("p h j d -> p h (j d)"),
-            )
+            for h in range(0, CHUNK_HEADS, STORE_HEADS):
+                first_head = half * CHUNK_HEADS + h
+                nc.sync.dma_start(
+                    out=outs[section][b, first_head : first_head + STORE_HEADS].rearrange(
+                        "h (p j) d -> p h (j d)", j=BLOCKS
+                    ),
+                    in_=result[:, h : h + STORE_HEADS].rearrange("p h j d -> p h (j d)"),
+                )
 
         def sum_squares(sums, j, features):
             squares = scratch.tile([P, CHUNK_HEADS, HEAD_DIM], F32)

@@ -25,7 +25,6 @@ BLOCKS = ROWS // P
 WORD_BLOCKS = FEATURES_IN // 2 // P
 HALVES = SECTION // ROWS
 CHUNK_HEADS = ROWS // HEAD_DIM
-STORE_HEADS = 4
 Q_SECTION, K_SECTION, V_SECTION = 0, 1, 2
 GROUPS_PER_HALF = 4
 MAX_SCALE_MUL = 100.0
@@ -44,7 +43,6 @@ def tile_selfattention_pa_kernel(
     nc = tc.nc
     outs = (out_0, out_1, out_2)
     with ExitStack() as ctx:
-        ctx.enter_context(tc.manual_schedule())
         keep = ctx.enter_context(tc.tile_pool(name="keep", bufs=1))
         stage = ctx.enter_context(tc.tile_pool(name="stage", bufs=4))
         scratch = ctx.enter_context(tc.tile_pool(name="scratch", bufs=2))
@@ -199,14 +197,13 @@ def tile_selfattention_pa_kernel(
             )
 
         def store(result, section, b, half):
-            for h in range(0, CHUNK_HEADS, STORE_HEADS):
-                first_head = half * CHUNK_HEADS + h
-                nc.sync.dma_start(
-                    out=outs[section][b, first_head : first_head + STORE_HEADS].rearrange(
-                        "h (p j) d -> p h (j d)", j=BLOCKS
-                    ),
-                    in_=result[:, h : h + STORE_HEADS].rearrange("p h j d -> p h (j d)"),
-                )
+            first_head = half * CHUNK_HEADS
+            nc.sync.dma_start(
+                out=outs[section][b, first_head : first_head + CHUNK_HEADS].rearrange(
+                    "h (p j) d -> p h (j d)", j=BLOCKS
+                ),
+                in_=result[:].rearrange("p h j d -> p h (j d)"),
+            )
 
         def sum_squares(sums, j, features):
             squares = scratch.tile([P, CHUNK_HEADS, HEAD_DIM], F32)

@@ -46,7 +46,7 @@ def tile_selfattention_pa_kernel(
         keep = ctx.enter_context(tc.tile_pool(name="keep", bufs=1))
         stage = ctx.enter_context(tc.tile_pool(name="stage", bufs=4))
         scratch = ctx.enter_context(tc.tile_pool(name="scratch", bufs=2))
-        results = ctx.enter_context(tc.tile_pool(name="results", bufs=6))
+        results = ctx.enter_context(tc.tile_pool(name="results", bufs=9))
         small = ctx.enter_context(tc.tile_pool(name="small", bufs=3))
         psum = ctx.enter_context(tc.psum_pool(name="psum", bufs=4))
 
@@ -73,22 +73,21 @@ def tile_selfattention_pa_kernel(
             codes.append(keep.tile([P, PASSES * ROWS], U32, name="codes%d" % i, align_bytes=64))
             scales.append(keep.tile([P, PASSES * ROWS], U8, name="scales%d" % i, align_bytes=64))
 
-        const_row = keep.tile([P, 2 * SECTION + ROWS], BF16)
-        nc.vector.memset(const_row[:], 0.0)
+        log_row = keep.tile([P, HEADS], BF16)
+        nc.vector.memset(log_row[:].bitcast(U32), 0)
         ones = keep.tile([P, P], BF16)
         nc.vector.memset(ones[:], 1.0)
+        q_row = keep.tile([P, SECTION], BF16)
+        nc.vector.memset(q_row[:].bitcast(U32), 0)
+        v_row = keep.tile([P, SECTION], BF16)
+        nc.vector.memset(v_row[:].bitcast(U32), 0)
         ident = keep.tile([P, P], F32)
         make_identity(nc, ident[:])
         nc.scalar.dma_start(
-            out=const_row[0:1, 0:SECTION], in_=q_bias.rearrange("(o n) -> o n", o=1)
+            out=log_row[0:1, :], in_=log_scale_mul.rearrange("o h a b -> o (h a b)")
         )
-        nc.scalar.dma_start(
-            out=const_row[0:1, SECTION : 2 * SECTION], in_=v_bias.rearrange("(o n) -> o n", o=1)
-        )
-        nc.scalar.dma_start(
-            out=const_row[0:1, 2 * SECTION : 2 * SECTION + HEADS],
-            in_=log_scale_mul.rearrange("o h a b -> o (h a b)"),
-        )
+        nc.scalar.dma_start(out=q_row[0:1, :], in_=q_bias.rearrange("(o n) -> o n", o=1))
+        nc.scalar.dma_start(out=v_row[0:1, :], in_=v_bias.rearrange("(o n) -> o n", o=1))
         warm = keep.tile([P, HEADS], F32)
         nc.scalar.activation(out=warm[:], in_=ones[:, 0:HEADS], func=ACT.Exp)
 
@@ -127,10 +126,10 @@ def tile_selfattention_pa_kernel(
                 ]
             copy(out=target, in_=flipped[(i, t)][:].rearrange("p (g u) c -> p g c u", u=2))
 
-        def flip(i, blocks, tag):
+        def flip(i, blocks, tag, copy=nc.scalar.copy):
             for t in blocks:
                 turn(i, t, tag)
-                collect(nc.scalar.copy, i, t)
+                collect(copy, i, t)
 
         def quantise(i, parts):
             width = PASSES * P if is_x(i) else ROWS
@@ -145,23 +144,18 @@ def tile_selfattention_pa_kernel(
         def quantise_all(i):
             quantise(i, range(BLOCKS if is_x(i) else PASSES))
 
-        bias = keep.tile([P, 2 * SECTION], F32)
         scale_mul = keep.tile([P, HEADS], F32)
 
-        def spread(i):
-            bank = psum.tile([P, ROWS], F32, tag="pass")
-            nc.tensor.matmul(
-                out=bank[:],
-                lhsT=ones[:],
-                rhs=const_row[:, i * ROWS : (i + 1) * ROWS],
-                start=True,
-                stop=True,
-            )
-            return bank
-
-        def spread_bias(i):
-            bank = spread(i)
-            nc.vector.tensor_copy(out=bias[:, i * ROWS : (i + 1) * ROWS], in_=bank[:])
+        def spread(row, name):
+            bank = psum.tile([P, SECTION], BF16, tag="pass")
+            for i in range(HALVES):
+                columns = slice(i * ROWS, (i + 1) * ROWS)
+                nc.tensor.matmul(
+                    out=bank[:, columns], lhsT=ones[:], rhs=row[:, columns], start=True, stop=True
+                )
+            bias = keep.tile([P, SECTION], BF16, name=name)
+            nc.vector.tensor_copy(out=bias[:], in_=bank[:])
+            return bias
 
         def products(b, section, half, tag):
             xg = x_group(b)
@@ -188,7 +182,7 @@ def tile_selfattention_pa_kernel(
             result = results.tile([P, CHUNK_HEADS, BLOCKS, HEAD_DIM], F32, tag="result")
             return result
 
-        def add_bias(result, j, acc, first_column):
+        def add_bias(result, j, acc, bias, first_column):
             nc.vector.tensor_tensor(
                 out=result[:, :, j, :],
                 in0=by_head(acc[:]),
@@ -196,13 +190,14 @@ def tile_selfattention_pa_kernel(
                 op=ALU.add,
             )
 
-        def store(result, section, b, half):
-            first_head = half * CHUNK_HEADS
+        def store(result, section, b, half, heads=slice(0, CHUNK_HEADS)):
+            first_head = half * CHUNK_HEADS + heads.start
+            count = heads.stop - heads.start
             nc.sync.dma_start(
-                out=outs[section][b, first_head : first_head + CHUNK_HEADS].rearrange(
+                out=outs[section][b, first_head : first_head + count].rearrange(
                     "h (p j) d -> p h (j d)", j=BLOCKS
                 ),
-                in_=result[:].rearrange("p h j d -> p h (j d)"),
+                in_=result[:, heads].rearrange("p h j d -> p h (j d)"),
             )
 
         def sum_squares(sums, j, features):
@@ -212,71 +207,74 @@ def tile_selfattention_pa_kernel(
                     out=squares[:, h, :],
                     in_=features[:, h, :],
                     func=ACT.Square,
-                    accum_out=sums[:, h, j : j + 1],
+                    accum_out=sums[:, j, h : h + 1],
                 )
-
-        def clamp(sums):
-            nc.vector.tensor_scalar_max(out=sums[:], in0=sums[:], scalar1=EPS * EPS)
 
         def root(sums):
-            nc.scalar.sqrt(out=sums[:], in_=sums[:])
+            nc.scalar.activation(out=sums, in_=sums, func=ACT.Abs_reciprocal_sqrt)
 
-        def invert(sums):
-            nc.vector.reciprocal(out=sums[:], in_=sums[:])
+        def scale_keys(k_result, waiting, j, heads=slice(0, CHUNK_HEADS)):
+            k_acc, k_sums, b, half = waiting
+            count = heads.stop - heads.start
+            nc.vector.scalar_tensor_tensor(
+                out=k_result[:, heads, j, :],
+                in0=k_sums[:, j, heads].unsqueeze(2).to_broadcast([P, count, HEAD_DIM]),
+                scalar=1.0 / EPS,
+                in1=by_head(k_acc[j][:])[:, heads],
+                op0=ALU.min,
+                op1=ALU.mult,
+            )
 
         def finish_keys(waiting):
-            k_acc, k_sums, b, half = waiting
             k_result = new_result()
-            invert(k_sums)
             for j in range(BLOCKS):
-                nc.vector.tensor_tensor(
-                    out=k_result[:, :, j, :],
-                    in0=by_head(k_acc[j][:]),
-                    in1=k_sums[:, :, j : j + 1].to_broadcast([P, CHUNK_HEADS, HEAD_DIM]),
-                    op=ALU.mult,
-                )
-            store(k_result, K_SECTION, b, half)
+                scale_keys(k_result, waiting, j)
+            store(k_result, K_SECTION, waiting[2], waiting[3])
 
         def scale_queries(q_result, q_sums, half):
             first_head = half * CHUNK_HEADS
-            invert(q_sums)
-            nc.vector.tensor_tensor(
+            nc.vector.scalar_tensor_tensor(
                 out=q_sums[:],
                 in0=q_sums[:],
+                scalar=1.0 / EPS,
                 in1=scale_mul[:, first_head : first_head + CHUNK_HEADS]
-                .unsqueeze(2)
-                .to_broadcast([P, CHUNK_HEADS, BLOCKS]),
-                op=ALU.mult,
+                .unsqueeze(1)
+                .to_broadcast([P, BLOCKS, CHUNK_HEADS]),
+                op0=ALU.min,
+                op1=ALU.mult,
             )
             for h in range(0, CHUNK_HEADS, 2):
-                two_heads = q_result[:, h : h + 2].rearrange("p h j d -> p (h j) d")
+                two_heads = q_result[:, h : h + 2]
                 nc.gpsimd.tensor_tensor(
                     out=two_heads,
                     in0=two_heads,
-                    in1=q_sums[:, h : h + 2]
-                    .rearrange("p h j -> p (h j)")
-                    .unsqueeze(2)
-                    .to_broadcast([P, 2 * BLOCKS, HEAD_DIM]),
+                    in1=q_sums[:, :, h : h + 2]
+                    .rearrange("p j h -> p h j")
+                    .unsqueeze(3)
+                    .to_broadcast([P, 2, BLOCKS, HEAD_DIM]),
                     op=ALU.mult,
                 )
 
-        flip(0, range(1), "pass")
+        log_bank = psum.tile([P, HEADS], F32, tag="pass")
+        nc.tensor.matmul(out=log_bank[:], lhsT=ones[:], rhs=log_row[:], start=True, stop=True)
+        nc.scalar.activation(out=scale_mul[:], in_=log_bank[:], func=ACT.Exp)
+        nc.scalar.activation(out=warm[:], in_=scale_mul[:], func=ACT.Abs_reciprocal_sqrt)
+        nc.gpsimd.tensor_scalar_min(out=scale_mul[:], in0=scale_mul[:], scalar1=MAX_SCALE_MUL)
+        flip(0, range(1), "pass", nc.vector.tensor_copy)
+        flip(1, range(3), "hold", nc.vector.tensor_copy)
+        flip(1, range(3, BLOCKS), "hold")
         quantise(0, range(1))
-        flip(1, range(BLOCKS), "hold")
-        spread_bias(0)
-        log_mul = spread(2 * SECTION // ROWS)
         flip(0, range(1, BLOCKS), "pass")
         quantise_all(1)
+        bias_q = spread(q_row, "bias_q")
         quantise(0, range(1, BLOCKS))
-        nc.scalar.activation(out=scale_mul[:], in_=log_mul[:, 0:HEADS], func=ACT.Exp)
-        nc.scalar.sqrt(out=warm[:], in_=scale_mul[:])
-        nc.gpsimd.tensor_scalar_min(out=scale_mul[:], in0=scale_mul[:], scalar1=MAX_SCALE_MUL)
 
         waiting = None
         scaling = None
         for n in range(BATCH * HALVES):
             half, b = divmod(n, BATCH)
             first_round = n == 0
+            last_round = n == BATCH * HALVES - 1
             ahead = [GROUPS_PER_HALF + 2 * n, GROUPS_PER_HALF + 2 * n + 1] if n < 2 else []
 
             q_acc = products(b, Q_SECTION, half, "pass")
@@ -285,51 +283,52 @@ def tile_selfattention_pa_kernel(
             if first_round:
                 for t in range(BLOCKS):
                     turn(2, t, "hold")
-            if waiting is not None:
-                clamp(waiting[1])
             q_result = new_result()
             for j in range(BLOCKS):
-                add_bias(q_result, j, q_acc[j], half * ROWS)
-            q_sums = small.tile([P, CHUNK_HEADS, BLOCKS], F32)
+                add_bias(q_result, j, q_acc[j], bias_q, half * ROWS)
+            q_sums = small.tile([P, BLOCKS, CHUNK_HEADS], F32)
             for j in range(BLOCKS):
                 sum_squares(q_sums, j, q_result[:, :, j, :])
-                if waiting is not None and j == 0:
-                    root(waiting[1])
             if first_round:
                 for t in range(BLOCKS):
                     collect(nc.vector.tensor_copy, 2, t)
                 quantise_all(2)
                 flip(3, range(BLOCKS), "pass")
-                for i in range(1, 2 * SECTION // ROWS):
-                    spread_bias(i)
+                bias_v = spread(v_row, "bias_v")
             if waiting is not None:
                 finish_keys(waiting)
 
             k_acc = products(b, K_SECTION, half, "hold")
-            clamp(q_sums)
+            root(q_sums[:])
             if first_round:
                 quantise_all(3)
             if n in (1, 2):
                 quantise_all(GROUPS_PER_HALF + 2 * n - 1)
             v_acc = products(b, V_SECTION, half, "pass")
-            k_sums = small.tile([P, CHUNK_HEADS, BLOCKS], F32)
+            scale_queries(q_result, q_sums, half)
+            k_sums = small.tile([P, BLOCKS, CHUNK_HEADS], F32)
+            waiting = (k_acc, k_sums, b, half)
+            k_result = new_result() if last_round else None
             for j in range(BLOCKS):
                 sum_squares(k_sums, j, by_head(k_acc[j][:]))
-                if j == 0:
-                    root(q_sums)
-            scale_queries(q_result, q_sums, half)
+                if last_round and j % 2:
+                    root(k_sums[:, j - 1 : j + 1, :])
             scaling = (q_result, b, half)
             v_result = new_result()
             for j in range(BLOCKS):
-                add_bias(v_result, j, v_acc[j], SECTION + half * ROWS)
+                add_bias(v_result, j, v_acc[j], bias_v, half * ROWS)
             store(v_result, V_SECTION, b, half)
+            if not last_round:
+                root(k_sums[:])
             for i in ahead:
                 flip(i, range(BLOCKS), "pass")
             if ahead:
                 quantise_all(ahead[0])
-            waiting = (k_acc, k_sums, b, half)
 
-        clamp(waiting[1])
-        root(waiting[1])
         store(scaling[0], Q_SECTION, scaling[1], scaling[2])
-        finish_keys(waiting)
+        for j in range(BLOCKS // 2):
+            scale_keys(k_result, waiting, j)
+        for heads in (slice(0, CHUNK_HEADS // 2), slice(CHUNK_HEADS // 2, CHUNK_HEADS)):
+            for j in range(BLOCKS // 2, BLOCKS):
+                scale_keys(k_result, waiting, j, heads)
+            store(k_result, K_SECTION, waiting[2], waiting[3], heads)

@@ -47,7 +47,7 @@ def tile_selfattention_pa_kernel(
         stage = ctx.enter_context(tc.tile_pool(name="stage", bufs=4))
         scratch = ctx.enter_context(tc.tile_pool(name="scratch", bufs=2))
         results = ctx.enter_context(tc.tile_pool(name="results", bufs=9))
-        small = ctx.enter_context(tc.tile_pool(name="small", bufs=3))
+        small = ctx.enter_context(tc.tile_pool(name="small", bufs=8))
         psum = ctx.enter_context(tc.psum_pool(name="psum", bufs=4))
 
         def x_group(b):
@@ -98,7 +98,7 @@ def tile_selfattention_pa_kernel(
         load(0, range(1))
         load(1, range(BLOCKS))
         load(0, range(1, BLOCKS))
-        for i in range(2, n_groups):
+        for i in (3, 4, 5, 2, 7, 6):
             load(i, range(BLOCKS))
 
         values = {}
@@ -233,15 +233,14 @@ def tile_selfattention_pa_kernel(
 
         def scale_queries(q_result, q_sums, half):
             first_head = half * CHUNK_HEADS
-            nc.vector.scalar_tensor_tensor(
+            nc.gpsimd.tensor_scalar_min(out=q_sums[:], in0=q_sums[:], scalar1=1.0 / EPS)
+            nc.gpsimd.tensor_tensor(
                 out=q_sums[:],
                 in0=q_sums[:],
-                scalar=1.0 / EPS,
                 in1=scale_mul[:, first_head : first_head + CHUNK_HEADS]
                 .unsqueeze(1)
                 .to_broadcast([P, BLOCKS, CHUNK_HEADS]),
-                op0=ALU.min,
-                op1=ALU.mult,
+                op=ALU.mult,
             )
             for h in range(0, CHUNK_HEADS, 2):
                 two_heads = q_result[:, h : h + 2]
@@ -255,80 +254,139 @@ def tile_selfattention_pa_kernel(
                     op=ALU.mult,
                 )
 
-        log_bank = psum.tile([P, HEADS], F32, tag="pass")
+        flip(0, range(1), "pass", nc.vector.tensor_copy)
+        for t in range(BLOCKS):
+            flip(1, [t], "hold", nc.scalar.copy if t % 2 else nc.vector.tensor_copy)
+        quantise(0, range(1))
+        quantise_all(1)
+        flip(0, range(1, BLOCKS), "pass")
+        log_bank = psum.tile([P, HEADS], F32, tag="hold")
         nc.tensor.matmul(out=log_bank[:], lhsT=ones[:], rhs=log_row[:], start=True, stop=True)
+        bias_q = spread(q_row, "bias_q")
+        quantise(0, range(1, BLOCKS))
         nc.scalar.activation(out=scale_mul[:], in_=log_bank[:], func=ACT.Exp)
         nc.scalar.activation(out=warm[:], in_=scale_mul[:], func=ACT.Abs_reciprocal_sqrt)
         nc.gpsimd.tensor_scalar_min(out=scale_mul[:], in0=scale_mul[:], scalar1=MAX_SCALE_MUL)
-        flip(0, range(1), "pass", nc.vector.tensor_copy)
-        flip(1, range(3), "hold", nc.vector.tensor_copy)
-        flip(1, range(3, BLOCKS), "hold")
-        quantise(0, range(1))
-        flip(0, range(1, BLOCKS), "pass")
-        quantise_all(1)
-        bias_q = spread(q_row, "bias_q")
-        quantise(0, range(1, BLOCKS))
 
-        waiting = None
-        scaling = None
-        for n in range(BATCH * HALVES):
-            half, b = divmod(n, BATCH)
-            first_round = n == 0
-            last_round = n == BATCH * HALVES - 1
-            ahead = [GROUPS_PER_HALF + 2 * n, GROUPS_PER_HALF + 2 * n + 1] if n < 2 else []
+        acc, result, sums = {}, {}, {}
 
-            q_acc = products(b, Q_SECTION, half, "pass")
-            if scaling is not None:
-                store(scaling[0], Q_SECTION, scaling[1], scaling[2])
-            if first_round:
-                for t in range(BLOCKS):
-                    turn(2, t, "hold")
-            q_result = new_result()
-            for j in range(BLOCKS):
-                add_bias(q_result, j, q_acc[j], bias_q, half * ROWS)
-            q_sums = small.tile([P, BLOCKS, CHUNK_HEADS], F32)
-            for j in range(BLOCKS):
-                sum_squares(q_sums, j, q_result[:, :, j, :])
-            if first_round:
-                for t in range(BLOCKS):
-                    collect(nc.vector.tensor_copy, 2, t)
-                quantise_all(2)
-                flip(3, range(BLOCKS), "pass")
-                bias_v = spread(v_row, "bias_v")
-            if waiting is not None:
-                finish_keys(waiting)
+        def multiply(kind, b, half, tag="pass"):
+            section = {"q": Q_SECTION, "k": K_SECTION, "v": V_SECTION}[kind]
+            acc[kind, b, half] = products(b, section, half, tag)
 
-            k_acc = products(b, K_SECTION, half, "hold")
-            root(q_sums[:])
-            if first_round:
-                quantise_all(3)
-            if n in (1, 2):
-                quantise_all(GROUPS_PER_HALF + 2 * n - 1)
-            v_acc = products(b, V_SECTION, half, "pass")
-            scale_queries(q_result, q_sums, half)
-            k_sums = small.tile([P, BLOCKS, CHUNK_HEADS], F32)
-            waiting = (k_acc, k_sums, b, half)
-            k_result = new_result() if last_round else None
+        def biased(kind, b, half):
+            key = kind, b, half
+            item = new_result()
+            result[key] = item
             for j in range(BLOCKS):
-                sum_squares(k_sums, j, by_head(k_acc[j][:]))
-                if last_round and j % 2:
-                    root(k_sums[:, j - 1 : j + 1, :])
-            scaling = (q_result, b, half)
-            v_result = new_result()
-            for j in range(BLOCKS):
-                add_bias(v_result, j, v_acc[j], bias_v, half * ROWS)
-            store(v_result, V_SECTION, b, half)
-            if not last_round:
-                root(k_sums[:])
-            for i in ahead:
-                flip(i, range(BLOCKS), "pass")
-            if ahead:
-                quantise_all(ahead[0])
+                add_bias(item, j, acc[key][j], bias_q if kind == "q" else bias_v, half * ROWS)
+            if kind == "v":
+                store(item, V_SECTION, b, half)
 
-        store(scaling[0], Q_SECTION, scaling[1], scaling[2])
-        for j in range(BLOCKS // 2):
+        def squares(kind, b, half, blocks):
+            key = kind, b, half
+            if key not in sums:
+                item = small.tile([P, BLOCKS, CHUNK_HEADS], F32, tag="sums")
+                sums[key] = item
+            for j in blocks:
+                if kind == "q":
+                    sum_squares(sums[key], j, result[key][:, :, j, :])
+                else:
+                    sum_squares(sums[key], j, by_head(acc[key][j][:]))
+
+        def finish_q(b, half):
+            root(sums["q", b, half][:])
+            scale_queries(result["q", b, half], sums["q", b, half], half)
+
+        def store_q(b, half):
+            store(result["q", b, half], Q_SECTION, b, half)
+
+        def finish_k(b, half):
+            finish_keys((acc["k", b, half], sums["k", b, half], b, half))
+
+        FIRST, SECOND = range(2), range(2, BLOCKS)
+        for t in range(BLOCKS):
+            flip(3, [t], "hold", nc.vector.tensor_copy if t in (3,) else nc.scalar.copy)
+        multiply("q", 0, 0)
+        biased("q", 0, 0)
+        quantise_all(3)
+        for t in range(BLOCKS):
+            flip(4, [t], "hold", nc.vector.tensor_copy if t in (3,) else nc.scalar.copy)
+        bias_v = spread(v_row, "bias_v")
+
+        multiply("v", 0, 0)
+        quantise_all(4)
+        biased("v", 0, 0)
+        squares("q", 0, 0, FIRST)
+        for t in range(BLOCKS):
+            flip(5, [t], "hold", nc.vector.tensor_copy if t in (3,) else nc.scalar.copy)
+
+        multiply("q", 1, 0)
+        quantise_all(5)
+        biased("q", 1, 0)
+        squares("q", 0, 0, SECOND)
+        for t in range(BLOCKS):
+            flip(2, [t], "hold", nc.vector.tensor_copy if t in (3,) else nc.scalar.copy)
+
+        multiply("v", 1, 0)
+        finish_q(0, 0)
+        quantise_all(2)
+        biased("v", 1, 0)
+        squares("q", 1, 0, FIRST)
+        for t in range(BLOCKS):
+            flip(7, [t], "hold", nc.vector.tensor_copy if t in (3,) else nc.scalar.copy)
+
+        multiply("q", 0, 1)
+        quantise_all(7)
+        biased("q", 0, 1)
+        squares("q", 1, 0, SECOND)
+        store_q(0, 0)
+        for t in range(BLOCKS):
+            flip(6, [t], "hold", nc.vector.tensor_copy if t in (3,) else nc.scalar.copy)
+
+        multiply("v", 0, 1)
+        finish_q(1, 0)
+        biased("v", 0, 1)
+        quantise_all(6)
+        squares("q", 0, 1, FIRST)
+        multiply("k", 0, 0, "hold")
+        multiply("q", 1, 1)
+        biased("q", 1, 1)
+        squares("q", 0, 1, SECOND)
+        store_q(1, 0)
+        multiply("v", 1, 1)
+        squares("k", 0, 0, range(1))
+        finish_q(0, 1)
+        biased("v", 1, 1)
+        squares("k", 0, 0, range(1, BLOCKS))
+        squares("q", 1, 1, range(1))
+        root(sums["k", 0, 0][:])
+        finish_k(0, 0)
+        multiply("k", 1, 0, "hold")
+        squares("q", 1, 1, range(1, BLOCKS))
+        store_q(0, 1)
+        multiply("k", 0, 1, "pass")
+        squares("k", 1, 0, range(1))
+        finish_q(1, 1)
+        squares("k", 1, 0, range(1, BLOCKS))
+        squares("k", 0, 1, range(1))
+        root(sums["k", 1, 0][:])
+        finish_k(1, 0)
+        multiply("k", 1, 1, "hold")
+        squares("k", 0, 1, range(1, BLOCKS))
+        store_q(1, 1)
+        squares("k", 1, 1, range(1))
+        root(sums["k", 0, 1][:])
+        finish_k(0, 1)
+        squares("k", 1, 1, range(1, 2))
+        root(sums["k", 1, 1][:, 0:2, :])
+        squares("k", 1, 1, SECOND)
+        root(sums["k", 1, 1][:, 2:4, :])
+        waiting = (acc["k", 1, 1], sums["k", 1, 1], 1, 1)
+        k_result = new_result()
+        for j in FIRST:
             scale_keys(k_result, waiting, j)
         for heads in (slice(0, CHUNK_HEADS // 2), slice(CHUNK_HEADS // 2, CHUNK_HEADS)):
-            for j in range(BLOCKS // 2, BLOCKS):
+            for j in SECOND:
                 scale_keys(k_result, waiting, j, heads)
-            store(k_result, K_SECTION, waiting[2], waiting[3], heads)
+            store(k_result, K_SECTION, 1, 1, heads)

@@ -142,7 +142,9 @@ def tile_selfattention_pa_kernel(
                 )
 
         def quantise_all(i):
-            quantise(i, range(BLOCKS if is_x(i) else PASSES))
+            nc.vector.quantize_mx(
+                out=codes[i][:].bitcast(FP8X4), scales=scales[i][:], in_=values[i][:]
+            )
 
         scale_mul = keep.tile([P, HEADS], F32)
 
@@ -258,7 +260,7 @@ def tile_selfattention_pa_kernel(
         for t in range(BLOCKS):
             flip(1, [t], "hold", nc.scalar.copy if t % 2 else nc.vector.tensor_copy)
         quantise(0, range(1))
-        quantise_all(1)
+        quantise(1, range(PASSES))
         flip(0, range(1, BLOCKS), "pass")
         log_bank = psum.tile([P, HEADS], F32, tag="hold")
         nc.tensor.matmul(out=log_bank[:], lhsT=ones[:], rhs=log_row[:], start=True, stop=True)
@@ -294,6 +296,33 @@ def tile_selfattention_pa_kernel(
                 else:
                     sum_squares(sums[key], j, by_head(acc[key][j][:]))
 
+        def squares_on_vector(b, half, blocks):
+            key = "k", b, half
+            if key not in sums:
+                item = small.tile([P, BLOCKS, CHUNK_HEADS], F32, tag="sums")
+                sums[key] = item
+            n = len(blocks)
+            stats = small.tile([P, n, CHUNK_HEADS, 3], F32, tag="stats%d" % n)
+            for i in range(n):
+                features = by_head(acc[key][blocks[i]][:])
+                for h in range(0, CHUNK_HEADS, 2):
+                    nc.vector.bn_stats(
+                        out=stats[:, i, h : h + 2, :].rearrange("p h c -> p (h c)"),
+                        in_=features[:, h : h + 2, :].rearrange("p h d -> p d h"),
+                    )
+            means = small.tile([P, n, CHUNK_HEADS], F32, tag="means%d" % n)
+            nc.vector.tensor_tensor(
+                out=means[:], in0=stats[:, :, :, 1], in1=stats[:, :, :, 1], op=ALU.mult
+            )
+            nc.vector.scalar_tensor_tensor(
+                out=sums[key][:, blocks[0] : blocks[0] + n, :],
+                in0=means[:],
+                scalar=float(HEAD_DIM),
+                in1=stats[:, :, :, 2],
+                op0=ALU.mult,
+                op1=ALU.add,
+            )
+
         def finish_q(b, half):
             root(sums["q", b, half][:])
             scale_queries(result["q", b, half], sums["q", b, half], half)
@@ -325,12 +354,13 @@ def tile_selfattention_pa_kernel(
         quantise_all(5)
         biased("q", 1, 0)
         squares("q", 0, 0, SECOND)
+        finish_q(0, 0)
         for t in range(BLOCKS):
             flip(2, [t], "hold", nc.vector.tensor_copy if t in (3,) else nc.scalar.copy)
 
         multiply("v", 1, 0)
-        finish_q(0, 0)
         quantise_all(2)
+        store_q(0, 0)
         biased("v", 1, 0)
         squares("q", 1, 0, FIRST)
         for t in range(BLOCKS):
@@ -340,12 +370,12 @@ def tile_selfattention_pa_kernel(
         quantise_all(7)
         biased("q", 0, 1)
         squares("q", 1, 0, SECOND)
-        store_q(0, 0)
+        finish_q(1, 0)
         for t in range(BLOCKS):
             flip(6, [t], "hold", nc.vector.tensor_copy if t in (3,) else nc.scalar.copy)
 
         multiply("v", 0, 1)
-        finish_q(1, 0)
+        store_q(1, 0)
         biased("v", 0, 1)
         quantise_all(6)
         squares("q", 0, 1, FIRST)
@@ -353,29 +383,29 @@ def tile_selfattention_pa_kernel(
         multiply("q", 1, 1)
         biased("q", 1, 1)
         squares("q", 0, 1, SECOND)
-        store_q(1, 0)
-        multiply("v", 1, 1)
-        squares("k", 0, 0, range(1))
         finish_q(0, 1)
+        multiply("v", 1, 1)
+        squares_on_vector(0, 0, range(2, BLOCKS))
+        squares("k", 0, 0, range(0, 2))
+        store_q(0, 1)
         biased("v", 1, 1)
-        squares("k", 0, 0, range(1, BLOCKS))
-        squares("q", 1, 1, range(1))
+        squares("q", 1, 1, range(2))
         root(sums["k", 0, 0][:])
         finish_k(0, 0)
-        multiply("k", 1, 0, "hold")
-        squares("q", 1, 1, range(1, BLOCKS))
-        store_q(0, 1)
-        multiply("k", 0, 1, "pass")
-        squares("k", 1, 0, range(1))
+        multiply("k", 1, 0, "pass")
+        squares("q", 1, 1, range(2, BLOCKS))
         finish_q(1, 1)
-        squares("k", 1, 0, range(1, BLOCKS))
-        squares("k", 0, 1, range(1))
+        multiply("k", 0, 1, "hold")
+        squares_on_vector(1, 0, range(3, BLOCKS))
+        squares("k", 1, 0, range(0, 3))
+        squares("k", 0, 1, range(0, 1))
         root(sums["k", 1, 0][:])
         finish_k(1, 0)
-        multiply("k", 1, 1, "hold")
-        squares("k", 0, 1, range(1, BLOCKS))
         store_q(1, 1)
-        squares("k", 1, 1, range(1))
+        multiply("k", 1, 1, "pass")
+        squares_on_vector(0, 1, range(3, BLOCKS))
+        squares("k", 0, 1, range(1, 3))
+        squares("k", 1, 1, range(0, 1))
         root(sums["k", 0, 1][:])
         finish_k(0, 1)
         squares("k", 1, 1, range(1, 2))

@@ -336,81 +336,77 @@ def tile_selfattention_pa_kernel(
         FIRST, SECOND = range(2), range(2, BLOCKS)
         for t in range(BLOCKS):
             flip(3, [t], "hold", nc.vector.tensor_copy if t in (3,) else nc.scalar.copy)
-        multiply("q", 0, 0)
+        multiply("q", 0, 0, "pass")
         biased("q", 0, 0)
+        squares("q", 0, 0, range(0, 2))
         quantise_all(3)
         for t in range(BLOCKS):
             flip(4, [t], "hold", nc.vector.tensor_copy if t in (3,) else nc.scalar.copy)
         bias_v = spread(v_row, "bias_v")
-
-        multiply("v", 0, 0)
+        multiply("v", 0, 0, "pass")
         quantise_all(4)
         biased("v", 0, 0)
-        squares("q", 0, 0, FIRST)
-        for t in range(BLOCKS):
-            flip(5, [t], "hold", nc.vector.tensor_copy if t in (3,) else nc.scalar.copy)
-
-        multiply("q", 1, 0)
-        quantise_all(5)
-        biased("q", 1, 0)
-        squares("q", 0, 0, SECOND)
+        squares("q", 0, 0, range(2, 4))
         finish_q(0, 0)
         for t in range(BLOCKS):
+            flip(5, [t], "hold", nc.vector.tensor_copy if t in (3,) else nc.scalar.copy)
+        multiply("q", 1, 0, "pass")
+        quantise_all(5)
+        biased("q", 1, 0)
+        for t in range(BLOCKS):
             flip(2, [t], "hold", nc.vector.tensor_copy if t in (3,) else nc.scalar.copy)
-
-        multiply("v", 1, 0)
+        squares("q", 1, 0, range(0, 1))
+        multiply("v", 1, 0, "pass")
         quantise_all(2)
         store_q(0, 0)
         biased("v", 1, 0)
-        squares("q", 1, 0, FIRST)
+        squares("q", 1, 0, range(1, 3))
         for t in range(BLOCKS):
             flip(7, [t], "hold", nc.vector.tensor_copy if t in (3,) else nc.scalar.copy)
-
-        multiply("q", 0, 1)
+        multiply("q", 0, 1, "pass")
         quantise_all(7)
         biased("q", 0, 1)
-        squares("q", 1, 0, SECOND)
+        squares("q", 1, 0, range(3, 4))
         finish_q(1, 0)
         for t in range(BLOCKS):
             flip(6, [t], "hold", nc.vector.tensor_copy if t in (3,) else nc.scalar.copy)
-
-        multiply("v", 0, 1)
+        multiply("v", 0, 1, "pass")
         store_q(1, 0)
         biased("v", 0, 1)
         quantise_all(6)
-        squares("q", 0, 1, FIRST)
+        squares("q", 0, 1, range(0, 2))
         multiply("k", 0, 0, "hold")
-        multiply("q", 1, 1)
+        multiply("q", 1, 1, "pass")
         biased("q", 1, 1)
-        squares("q", 0, 1, SECOND)
+        squares("q", 0, 1, range(2, 4))
         finish_q(0, 1)
-        multiply("v", 1, 1)
-        squares_on_vector(0, 0, range(2, BLOCKS))
+        multiply("v", 1, 1, "pass")
+        squares_on_vector(0, 0, range(2, 4))
         squares("k", 0, 0, range(0, 2))
         store_q(0, 1)
         biased("v", 1, 1)
-        squares("q", 1, 1, range(2))
+        squares("q", 1, 1, range(0, 2))
         root(sums["k", 0, 0][:])
         finish_k(0, 0)
         multiply("k", 1, 0, "pass")
-        squares("q", 1, 1, range(2, BLOCKS))
+        squares("q", 1, 1, range(2, 4))
         finish_q(1, 1)
         multiply("k", 0, 1, "hold")
-        squares_on_vector(1, 0, range(3, BLOCKS))
+        squares_on_vector(1, 0, range(3, 4))
         squares("k", 1, 0, range(0, 3))
         squares("k", 0, 1, range(0, 1))
+        store_q(1, 1)
         root(sums["k", 1, 0][:])
         finish_k(1, 0)
-        store_q(1, 1)
         multiply("k", 1, 1, "pass")
-        squares_on_vector(0, 1, range(3, BLOCKS))
+        squares_on_vector(0, 1, range(3, 4))
         squares("k", 0, 1, range(1, 3))
         squares("k", 1, 1, range(0, 1))
         root(sums["k", 0, 1][:])
         finish_k(0, 1)
         squares("k", 1, 1, range(1, 2))
         root(sums["k", 1, 1][:, 0:2, :])
-        squares("k", 1, 1, SECOND)
+        squares("k", 1, 1, range(2, 4))
         root(sums["k", 1, 1][:, 2:4, :])
         waiting = (acc["k", 1, 1], sums["k", 1, 1], 1, 1)
         k_result = new_result()

from contextlib import ExitStack

import concourse.mybir as mybir
from concourse.masks import make_identity

F32 = mybir.dt.float32
BF16 = mybir.dt.bfloat16
U32 = mybir.dt.uint32
U8 = mybir.dt.uint8
FP8X4 = mybir.dt.float8_e4m3fn_x4
ALU = mybir.AluOpType
ACT = mybir.ActivationFunctionType

P = 128
BATCH = 2
FEATURES_IN = 1024
HEADS = 16
HEAD_DIM = 64
SECTION = HEADS * HEAD_DIM
PACK = 4
K_PASS = P * PACK
PASSES = FEATURES_IN // K_PASS
ROWS = 512
BLOCKS = ROWS // P
WORD_BLOCKS = FEATURES_IN // 2 // P
HALVES = SECTION // ROWS
CHUNK_HEADS = ROWS // HEAD_DIM
Q_SECTION, K_SECTION, V_SECTION = 0, 1, 2
GROUPS_PER_HALF = 4
MAX_SCALE_MUL = 100.0
EPS = 1e-12

FLOPS = 2 * BATCH * ROWS * FEATURES_IN * 3 * SECTION


def by_head(columns):
    return columns.rearrange("p (h d) -> p h d", d=HEAD_DIM)


def tile_selfattention_pa_kernel(
    tc, x, W_qkv, q_bias, v_bias, log_scale_mul, out_0, out_1, out_2
):
    nc = tc.nc
    outs = (out_0, out_1, out_2)
    with ExitStack() as ctx:
        keep = ctx.enter_context(tc.tile_pool(name="keep", bufs=1))
        stage = ctx.enter_context(tc.tile_pool(name="stage", bufs=4))
        scratch = ctx.enter_context(tc.tile_pool(name="scratch", bufs=2))
        results = ctx.enter_context(tc.tile_pool(name="results", bufs=9))
        small = ctx.enter_context(tc.tile_pool(name="small", bufs=8))
        psum = ctx.enter_context(tc.psum_pool(name="psum", bufs=4))

        def x_group(b):
            return b * GROUPS_PER_HALF

        def w_group(section, half):
            return half * GROUPS_PER_HALF + 1 + section

        def is_x(i):
            return i % GROUPS_PER_HALF == 0

        def source(i):
            half, kind = divmod(i, GROUPS_PER_HALF)
            if is_x(i):
                return x[half].rearrange("(p j) k -> p j k", j=BLOCKS)
            first = (kind - 1) * SECTION + half * ROWS
            return W_qkv[first : first + ROWS, :].rearrange("(t p) k -> p t k", p=P)

        n_groups = BATCH * GROUPS_PER_HALF
        raw, codes, scales = [], [], []
        for i in range(n_groups):
            raw.append(keep.tile([P, BLOCKS, FEATURES_IN], BF16, name="raw%d" % i))
            codes.append(keep.tile([P, PASSES * ROWS], U32, name="codes%d" % i, align_bytes=64))
            scales.append(keep.tile([P, PASSES * ROWS], U8, name="scales%d" % i, align_bytes=64))

        log_row = keep.tile([P, HEADS], BF16)
        nc.vector.memset(log_row[:].bitcast(U32), 0)
        ones = keep.tile([P, P], BF16)
        nc.vector.memset(ones[:], 1.0)
        q_row = keep.tile([P, SECTION], BF16)
        nc.vector.memset(q_row[:].bitcast(U32), 0)
        v_row = keep.tile([P, SECTION], BF16)
        nc.vector.memset(v_row[:].bitcast(U32), 0)
        ident = keep.tile([P, P], F32)
        make_identity(nc, ident[:])
        nc.scalar.dma_start(
            out=log_row[0:1, :], in_=log_scale_mul.rearrange("o h a b -> o (h a b)")
        )
        nc.scalar.dma_start(out=q_row[0:1, :], in_=q_bias.rearrange("(o n) -> o n", o=1))
        nc.scalar.dma_start(out=v_row[0:1, :], in_=v_bias.rearrange("(o n) -> o n", o=1))
        warm = keep.tile([P, HEADS], F32)
        nc.scalar.activation(out=warm[:], in_=ones[:, 0:HEADS], func=ACT.Exp)

        def load(i, blocks):
            for t in blocks:
                nc.sync.dma_start(out=raw[i][:, t, :], in_=source(i)[:, t, :])

        load(0, range(1))
        load(1, range(BLOCKS))
        load(0, range(1, BLOCKS))
        for i in (3, 4, 5, 2, 7, 6):
            load(i, range(BLOCKS))

        values = {}
        flipped = {}

        def turn(i, t, tag):
            if i not in values:
                values[i] = stage.tile(
                    [P, PASSES * ROWS * PACK], BF16, name="values%d" % i, tag="values", align_bytes=64
                )
            raw_words = raw[i][:].bitcast(F32)
            bank = psum.tile([P, WORD_BLOCKS, P], F32, tag=tag)
            for gu in range(WORD_BLOCKS):
                columns = slice(gu * P, (gu + 1) * P)
                nc.tensor.transpose(bank[:, gu, :], raw_words[:, t, columns], ident[:])
            flipped[(i, t)] = bank

        def collect(copy, i, t):
            words = values[i][:].bitcast(F32)
            if is_x(i):
                target = words.rearrange("p (t g c u) -> p t g c u", t=BLOCKS, g=PASSES, u=2)[:, t]
            else:
                target = words.rearrange("p (g c u) -> p g c u", g=PASSES, u=2)[
                    :, :, t * P : (t + 1) * P, :
                ]
            copy(out=target, in_=flipped[(i, t)][:].rearrange("p (g u) c -> p g c u", u=2))

        def flip(i, blocks, tag, copy=nc.scalar.copy):
            for t in blocks:
                turn(i, t, tag)
                collect(copy, i, t)

        def quantise(i, parts):
            width = PASSES * P if is_x(i) else ROWS
            for part in parts:
                words = slice(part * width, (part + 1) * width)
                nc.vector.quantize_mx(
                    out=codes[i][:, words].bitcast(FP8X4),
                    scales=scales[i][:, words],
                    in_=values[i][:, part * width * PACK : (part + 1) * width * PACK],
                )

        def quantise_all(i):
            nc.vector.quantize_mx(
                out=codes[i][:].bitcast(FP8X4), scales=scales[i][:], in_=values[i][:]
            )

        scale_mul = keep.tile([P, HEADS], F32)

        def spread(row, name):
            bank = psum.tile([P, SECTION], BF16, tag="pass")
            for i in range(HALVES):
                columns = slice(i * ROWS, (i + 1) * ROWS)
                nc.tensor.matmul(
                    out=bank[:, columns], lhsT=ones[:], rhs=row[:, columns], start=True, stop=True
                )
            bias = keep.tile([P, SECTION], BF16, name=name)
            nc.vector.tensor_copy(out=bias[:], in_=bank[:])
            return bias

        def products(b, section, half, tag):
            xg = x_group(b)
            wg = w_group(section, half)
            banks = []
            for j in range(BLOCKS):
                acc = psum.tile([P, ROWS], F32, tag=tag)
                for g in range(PASSES):
                    tokens = slice((j * PASSES + g) * P, (j * PASSES + g + 1) * P)
                    features = slice(g * ROWS, (g + 1) * ROWS)
                    nc.tensor.matmul_mx(
                        out=acc[:],
                        lhsT=codes[xg][:, tokens].bitcast(FP8X4),
                        lhsT_scale=scales[xg][:, tokens],
                        rhs=codes[wg][:, features].bitcast(FP8X4),
                        rhs_scale=scales[wg][:, features],
                        start=(g == 0),
                        stop=(g == PASSES - 1),
                    )
                banks.append(acc)
            return banks

        def new_result():
            result = results.tile([P, CHUNK_HEADS, BLOCKS, HEAD_DIM], F32, tag="result")
            return result

        def add_bias(result, j, acc, bias, first_column):
            nc.vector.tensor_tensor(
                out=result[:, :, j, :],
                in0=by_head(acc[:]),
                in1=by_head(bias[:, first_column : first_column + ROWS]),
                op=ALU.add,
            )

        def store(result, section, b, half, heads=slice(0, CHUNK_HEADS)):
            first_head = half * CHUNK_HEADS + heads.start
            count = heads.stop - heads.start
            nc.sync.dma_start(
                out=outs[section][b, first_head : first_head + count].rearrange(
                    "h (p j) d -> p h (j d)", j=BLOCKS
                ),
                in_=result[:, heads].rearrange("p h j d -> p h (j d)"),
            )

        def sum_squares(sums, j, features):
            squares = scratch.tile([P, CHUNK_HEADS, HEAD_DIM], F32)
            for h in range(CHUNK_HEADS):
                nc.scalar.activation(
                    out=squares[:, h, :],
                    in_=features[:, h, :],
                    func=ACT.Square,
                    accum_out=sums[:, j, h : h + 1],
                )

        def root(sums):
            nc.scalar.activation(out=sums, in_=sums, func=ACT.Abs_reciprocal_sqrt)

        def scale_keys(k_result, waiting, j, heads=slice(0, CHUNK_HEADS)):
            k_acc, k_sums, b, half = waiting
            count = heads.stop - heads.start
            nc.vector.scalar_tensor_tensor(
                out=k_result[:, heads, j, :],
                in0=k_sums[:, j, heads].unsqueeze(2).to_broadcast([P, count, HEAD_DIM]),
                scalar=1.0 / EPS,
                in1=by_head(k_acc[j][:])[:, heads],
                op0=ALU.min,
                op1=ALU.mult,
            )

        def finish_keys(waiting):
            k_result = new_result()
            for j in range(BLOCKS):
                scale_keys(k_result, waiting, j)
            store(k_result, K_SECTION, waiting[2], waiting[3])

        def scale_queries(q_result, q_sums, half):
            first_head = half * CHUNK_HEADS
            nc.gpsimd.tensor_scalar_min(out=q_sums[:], in0=q_sums[:], scalar1=1.0 / EPS)
            nc.gpsimd.tensor_tensor(
                out=q_sums[:],
                in0=q_sums[:],
                in1=scale_mul[:, first_head : first_head + CHUNK_HEADS]
                .unsqueeze(1)
                .to_broadcast([P, BLOCKS, CHUNK_HEADS]),
                op=ALU.mult,
            )
            for h in range(0, CHUNK_HEADS, 2):
                two_heads = q_result[:, h : h + 2]
                nc.gpsimd.tensor_tensor(
                    out=two_heads,
                    in0=two_heads,
                    in1=q_sums[:, :, h : h + 2]
                    .rearrange("p j h -> p h j")
                    .unsqueeze(3)
                    .to_broadcast([P, 2, BLOCKS, HEAD_DIM]),
                    op=ALU.mult,
                )

        flip(0, range(1), "pass", nc.vector.tensor_copy)
        for t in range(BLOCKS):
            flip(1, [t], "hold", nc.scalar.copy if t % 2 else nc.vector.tensor_copy)
        quantise(0, range(1))
        quantise(1, range(PASSES))
        flip(0, range(1, BLOCKS), "pass")
        log_bank = psum.tile([P, HEADS], F32, tag="hold")
        nc.tensor.matmul(out=log_bank[:], lhsT=ones[:], rhs=log_row[:], start=True, stop=True)
        bias_q = spread(q_row, "bias_q")
        quantise(0, range(1, BLOCKS))
        nc.scalar.activation(out=scale_mul[:], in_=log_bank[:], func=ACT.Exp)
        nc.scalar.activation(out=warm[:], in_=scale_mul[:], func=ACT.Abs_reciprocal_sqrt)
        nc.gpsimd.tensor_scalar_min(out=scale_mul[:], in0=scale_mul[:], scalar1=MAX_SCALE_MUL)

        acc, result, sums = {}, {}, {}

        def multiply(kind, b, half, tag="pass"):
            section = {"q": Q_SECTION, "k": K_SECTION, "v": V_SECTION}[kind]
            acc[kind, b, half] = products(b, section, half, tag)

        def biased(kind, b, half):
            key = kind, b, half
            item = new_result()
            result[key] = item
            for j in range(BLOCKS):
                add_bias(item, j, acc[key][j], bias_q if kind == "q" else bias_v, half * ROWS)
            if kind == "v":
                store(item, V_SECTION, b, half)

        def squares(kind, b, half, blocks):
            key = kind, b, half
            if key not in sums:
                item = small.tile([P, BLOCKS, CHUNK_HEADS], F32, tag="sums")
                sums[key] = item
            for j in blocks:
                if kind == "q":
                    sum_squares(sums[key], j, result[key][:, :, j, :])
                else:
                    sum_squares(sums[key], j, by_head(acc[key][j][:]))

        def squares_on_vector(b, half, blocks):
            key = "k", b, half
            if key not in sums:
                item = small.tile([P, BLOCKS, CHUNK_HEADS], F32, tag="sums")
                sums[key] = item
            n = len(blocks)
            stats = small.tile([P, n, CHUNK_HEADS, 3], F32, tag="stats%d" % n)
            for i in range(n):
                features = by_head(acc[key][blocks[i]][:])
                for h in range(0, CHUNK_HEADS, 2):
                    nc.vector.bn_stats(
                        out=stats[:, i, h : h + 2, :].rearrange("p h c -> p (h c)"),
                        in_=features[:, h : h + 2, :].rearrange("p h d -> p d h"),
                    )
            means = small.tile([P, n, CHUNK_HEADS], F32, tag="means%d" % n)
            nc.vector.tensor_tensor(
                out=means[:], in0=stats[:, :, :, 1], in1=stats[:, :, :, 1], op=ALU.mult
            )
            nc.vector.scalar_tensor_tensor(
                out=sums[key][:, blocks[0] : blocks[0] + n, :],
                in0=means[:],
                scalar=float(HEAD_DIM),
                in1=stats[:, :, :, 2],
                op0=ALU.mult,
                op1=ALU.add,
            )

        def finish_q(b, half):
            root(sums["q", b, half][:])
            scale_queries(result["q", b, half], sums["q", b, half], half)

        def store_q(b, half):
            store(result["q", b, half], Q_SECTION, b, half)

        def finish_k(b, half):
            finish_keys((acc["k", b, half], sums["k", b, half], b, half))

        FIRST, SECOND = range(2), range(2, BLOCKS)
        for t in range(BLOCKS):
            flip(3, [t], "hold", nc.vector.tensor_copy if t in (3,) else nc.scalar.copy)
        multiply("q", 0, 0, "pass")
        biased("q", 0, 0)
        squares("q", 0, 0, range(0, 2))
        quantise_all(3)
        for t in range(BLOCKS):
            flip(4, [t], "hold", nc.vector.tensor_copy if t in (3,) else nc.scalar.copy)
        bias_v = spread(v_row, "bias_v")
        multiply("v", 0, 0, "pass")
        quantise_all(4)
        biased("v", 0, 0)
        squares("q", 0, 0, range(2, 4))
        finish_q(0, 0)
        for t in range(BLOCKS):
            flip(5, [t], "hold", nc.vector.tensor_copy if t in (3,) else nc.scalar.copy)
        multiply("q", 1, 0, "pass")
        quantise_all(5)
        biased("q", 1, 0)
        for t in range(BLOCKS):
            flip(2, [t], "hold", nc.vector.tensor_copy if t in (3,) else nc.scalar.copy)
        squares("q", 1, 0, range(0, 1))
        multiply("v", 1, 0, "pass")
        quantise_all(2)
        store_q(0, 0)
        biased("v", 1, 0)
        squares("q", 1, 0, range(1, 3))
        for t in range(BLOCKS):
            flip(7, [t], "hold", nc.vector.tensor_copy if t in (3,) else nc.scalar.copy)
        multiply("q", 0, 1, "pass")
        quantise_all(7)
        biased("q", 0, 1)
        squares("q", 1, 0, range(3, 4))
        finish_q(1, 0)
        for t in range(BLOCKS):
            flip(6, [t], "hold", nc.vector.tensor_copy if t in (3,) else nc.scalar.copy)
        multiply("v", 0, 1, "pass")
        store_q(1, 0)
        biased("v", 0, 1)
        quantise_all(6)
        squares("q", 0, 1, range(0, 2))
        multiply("k", 0, 0, "hold")
        multiply("q", 1, 1, "pass")
        biased("q", 1, 1)
        squares("q", 0, 1, range(2, 4))
        finish_q(0, 1)
        multiply("v", 1, 1, "pass")
        squares_on_vector(0, 0, range(2, 4))
        squares("k", 0, 0, range(0, 2))
        store_q(0, 1)
        biased("v", 1, 1)
        squares("q", 1, 1, range(0, 2))
        root(sums["k", 0, 0][:])
        finish_k(0, 0)
        multiply("k", 1, 0, "pass")
        squares("q", 1, 1, range(2, 4))
        finish_q(1, 1)
        multiply("k", 0, 1, "hold")
        squares_on_vector(1, 0, range(3, 4))
        squares("k", 1, 0, range(0, 3))
        squares("k", 0, 1, range(0, 1))
        store_q(1, 1)
        root(sums["k", 1, 0][:])
        finish_k(1, 0)
        multiply("k", 1, 1, "pass")
        squares_on_vector(0, 1, range(3, 4))
        squares("k", 0, 1, range(1, 3))
        squares("k", 1, 1, range(0, 1))
        root(sums["k", 0, 1][:])
        finish_k(0, 1)
        squares("k", 1, 1, range(1, 2))
        root(sums["k", 1, 1][:, 0:2, :])
        squares("k", 1, 1, range(2, 4))
        root(sums["k", 1, 1][:, 2:4, :])
        waiting = (acc["k", 1, 1], sums["k", 1, 1], 1, 1)
        k_result = new_result()
        for j in FIRST:
            scale_keys(k_result, waiting, j)
        for heads in (slice(0, CHUNK_HEADS // 2), slice(CHUNK_HEADS // 2, CHUNK_HEADS)):
            for j in SECOND:
                scale_keys(k_result, waiting, j, heads)
            store(k_result, K_SECTION, 1, 1, heads)
